import numpy as np
import ml_dtypes


def mxq(x, axis, fmt="e4m3"):
    dtype, down = {"e4m3": (ml_dtypes.float8_e4m3fn, 7), "e5m2": (ml_dtypes.float8_e5m2, 14)}[fmt]
    v = np.moveaxis(np.asarray(x, np.float32).astype(ml_dtypes.bfloat16).astype(np.float64), axis, -1)
    blocks = v.reshape(v.shape[:-1] + (-1, 32))
    amax = np.abs(blocks).max(-1, keepdims=True)
    byte = np.maximum(np.where(amax > 0, np.frexp(amax)[1] - 1 + 127, 0) - down, 1)
    scale = np.exp2(byte - 127.0)
    codes = (blocks / scale).astype(np.float32).astype(dtype).astype(np.float64)
    return np.moveaxis((codes * scale).reshape(v.shape), -1, axis)


WIDE = False


def mx_kscale(k):
    if not WIDE:
        return np.ones(k)
    levels = np.array([10, -10, 5, -5, 0])
    a = np.random.permutation(np.resize(levels, k // 512 * 4)).reshape(k // 512, 4)
    idx = np.arange(k)
    return np.exp2(a[idx // 512, idx % 128 // 32])


BF16 = ml_dtypes.bfloat16


def bf(x):
    return np.asarray(x, np.float32).astype(BF16)


def f64(x):
    return np.asarray(x).astype(np.float64)


B, K, L, D, H = 8, 8, 512, 256, 128


def erf(v):
    c = np.clip(v, -6.0, 6.0)
    q = 2.0 * c * c
    term = c.copy()
    total = c.copy()
    for n in range(1, 120):
        term = term * q / (2.0 * n + 1.0)
        total = total + term
    return 2.0 / np.sqrt(np.pi) * np.exp(-c * c) * total


def gelu_erf(v):
    return 0.5 * v * (1.0 + erf(v / np.sqrt(2.0)))


def sigmoid(v):
    return 1.0 / (1.0 + np.exp(-v))


def setup_inputs():
    t = mx_kscale(2 * D)[D:]
    wf = np.random.standard_normal((2 * D, D)) / np.sqrt(2 * D)
    wf[D:] = wf[D:] / t[:, None]
    return {
        "orig_feat": bf(np.random.standard_normal((B, L, D))),
        "rag_feat": bf(np.random.standard_normal((B, K, L, D)) * t),
        "af": bf(np.random.uniform(0.01, 0.99, (B, L))),
        "h_af": bf(np.maximum(np.random.standard_normal((B, L, H)), 0.0) * np.random.uniform(0.0, 1.0, (B, L, 1))),
        "w2": bf(np.random.standard_normal((H, D)) * 2.0 / np.sqrt(H)),
        "b2": bf(-np.log(D / 2.0) + 0.3 * np.random.standard_normal(D)),
        "wf": bf(wf),
        "bias_f": bf(np.random.standard_normal(D) * 0.5),
        "ln_g": bf(1.0 + 0.2 * np.random.standard_normal(D)),
        "ln_b": bf(0.3 * np.random.standard_normal(D)),
    }


def reference(orig_feat, rag_feat, af, h_af, w2, b2, wf, bias_f, ln_g, ln_b):
    o, r, a = f64(orig_feat), f64(rag_feat), f64(af)
    af_weight = sigmoid(f64(h_af) @ f64(w2) + f64(b2))
    s = af_weight.sum(-1)
    pooled_ref = (0.7 * r.mean(axis=1) + 0.3 * r.max(axis=1)) * s[:, :, None]
    x = np.concatenate([o, pooled_ref], axis=-1)
    y = (mxq(x, 2, "e4m3") @ mxq(f64(wf), 0, "e4m3")) + f64(bias_f)
    mu = y.mean(-1, keepdims=True)
    var = ((y - mu) ** 2).mean(-1, keepdims=True)
    yn = (y - mu) / np.sqrt(var + 1e-5) * f64(ln_g) + f64(ln_b)
    fused = gelu_erf(yn)
    return o + fused * np.sqrt(a * (1.0 - a))[..., None]

@@ -1,0 +1,285 @@
+from contextlib import ExitStack
+
+import concourse.mybir as mybir
+from concourse.masks import make_identity
+
+FLOPS = 2 * 4096 * 128 * 256 + 2 * 4096 * 512 * 256
+
+F32 = mybir.dt.float32
+BF16 = mybir.dt.bfloat16
+U32 = mybir.dt.uint32
+U8 = mybir.dt.uint8
+FP8X4 = mybir.dt.float8_e4m3fn_x4
+ALU = mybir.AluOpType
+ACT = mybir.ActivationFunctionType
+
+P = 128
+NB = 8
+NK = 8
+D = 256
+KV = 5
+
+
+def tile_rarevariantawarefusion_pa_t_kernel(
+    tc, orig_feat, rag_feat, af, h_af, w2, b2, wf, bias_f, ln_g, ln_b, out
+):
+    nc = tc.nc
+    with ExitStack() as ctx:
+        const = ctx.enter_context(tc.tile_pool(name="const", bufs=1))
+        s1 = ctx.enter_context(tc.tile_pool(name="s1", bufs=2))
+        rpool = ctx.enter_context(tc.tile_pool(name="rpool", bufs=5))
+        fpool = ctx.enter_context(tc.tile_pool(name="fpool", bufs=3))
+        work = ctx.enter_context(tc.tile_pool(name="work", bufs=3))
+        tiny = ctx.enter_context(tc.tile_pool(name="tiny", bufs=4))
+        psum = ctx.enter_context(tc.psum_pool(name="psum", bufs=1))
+
+        h_sb = const.tile([P, NB, 4, 128], BF16, name="h_sb")
+        nc.sync.dma_start(
+            out=h_sb[:].rearrange("p b c h -> p b (c h)"),
+            in_=h_af.rearrange("b (i c) h -> i b (c h)", c=4),
+        )
+        w2_sb = const.tile([P, D], BF16, name="w2_sb")
+        nc.scalar.dma_start(out=w2_sb[:], in_=w2)
+        vrow = const.tile([P, P], BF16, name="vrow")
+        nc.vector.memset(vrow[:], 0.0)
+        nc.scalar.dma_start(out=vrow[0:2, :], in_=b2.rearrange("(r c) -> r c", r=2))
+        nc.scalar.dma_start(out=vrow[2:4, :], in_=ln_g.rearrange("(r c) -> r c", r=2))
+        nc.scalar.dma_start(out=vrow[4:6, :], in_=ln_b.rearrange("(r c) -> r c", r=2))
+
+        ident_b = const.tile([P, P], BF16, name="ident_b")
+        make_identity(nc, ident_b[:])
+        ident_f = const.tile([P, P], F32, name="ident_f")
+        make_identity(nc, ident_f[:])
+        ones_f = const.tile([P, 2], F32, name="ones_f")
+        nc.vector.memset(ones_f[:], 1.0)
+        half_p = const.tile([P, 32], F32, name="half_p")
+        nc.vector.memset(half_p[:], 0.5)
+        half_n = const.tile([P, 2], F32, name="half_n")
+        nc.vector.memset(half_n[:], -0.5)
+
+        wst = const.tile([P, 2, 4, 512], BF16, name="wst")
+        nc.vector.memset(wst[:], 0.0)
+        top = wf[0:256, :].rearrange("(j t) n -> j t n", t=4)
+        bot = wf[256:512, :].rearrange("(j t) n -> j t n", t=4)
+        nc.scalar.dma_start(out=wst[0:64, 0, :, 0:256], in_=top)
+        nc.scalar.dma_start(out=wst[64:128, 0, :, 256:512], in_=top)
+        nc.scalar.dma_start(out=wst[0:64, 1, :, 256:512], in_=bot)
+        nc.scalar.dma_start(out=wst[64:128, 1, :, 0:256], in_=bot)
+        bias_bc = const.tile([P, D], BF16, name="bias_bc")
+        nc.scalar.dma_start(out=bias_bc[:], in_=bias_f.partition_broadcast(P))
+        a_bf = const.tile([P, NB, 4], BF16, name="a_bf")
+        nc.scalar.dma_start(out=a_bf[:], in_=af.rearrange("b (i c) -> i b c", c=4))
+
+        vt_ps = psum.tile([P, P], BF16, tag="f", bufs=2, name="vt_ps")
+        nc.tensor.transpose(vt_ps[:], vrow[:], ident_b[:])
+        vcol = const.tile([P, 8], F32, name="vcol")
+        nc.vector.tensor_copy(out=vcol[:, 0:6], in_=vt_ps[:, 0:6])
+
+        sc1 = const.tile([P, 32], F32, name="sc1")
+        sc2 = const.tile([P, 32], F32, name="sc2")
+        for b in range(NB):
+            ht_ps = psum.tile([P, 4, 128], BF16, tag="o", bufs=1, name="ht_ps")
+            for c in range(4):
+                nc.tensor.transpose(ht_ps[:, c, :], h_sb[:, b, c, :], ident_b[:])
+            ht = s1.tile([P, 512], BF16, name="ht")
+            nc.vector.tensor_copy(out=ht[:], in_=ht_ps[:].rearrange("p c i -> p (c i)"))
+            sig = s1.tile([P, 2, 512], F32, name="sig")
+            for dh in range(2):
+                z_ps = psum.tile([P, 512], F32, tag="acc", bufs=2, name="z_ps")
+                nc.tensor.matmul(
+                    z_ps[:], lhsT=w2_sb[:, dh * 128 : (dh + 1) * 128], rhs=ht[:], start=True, stop=True
+                )
+                nc.scalar.activation(
+                    out=sig[:, dh, :], in_=z_ps[:], func=ACT.Sigmoid, bias=vcol[:, dh : dh + 1]
+                )
+            s_ps = psum.tile([P, 4], F32, tag="zt", bufs=1, name="s_ps")
+            for c in range(4):
+                for dh in range(2):
+                    nc.tensor.matmul(
+                        s_ps[:, c : c + 1],
+                        lhsT=sig[:, dh, c * 128 : (c + 1) * 128],
+                        rhs=ones_f[:, 0:1],
+                        start=(dh == 0),
+                        stop=(dh == 1),
+                    )
+            nc.vector.tensor_scalar(
+                out=sc1[:, b * 4 : (b + 1) * 4], in0=s_ps[:], scalar1=0.7 / 8.0, scalar2=None, op0=ALU.mult
+            )
+            nc.vector.tensor_scalar(
+                out=sc2[:, b * 4 : (b + 1) * 4], in0=s_ps[:], scalar1=0.3, scalar2=None, op0=ALU.mult
+            )
+
+        wg = const.tile([P, 2, 512, 4], BF16, name="wg", align_bytes=64)
+        wc = const.tile([P, 2, 512], U32, name="wc", align_bytes=64)
+        ws = const.tile([P, 2, 512], U8, name="ws", align_bytes=64)
+        for g in range(2):
+            nc.vector.tensor_copy(out=wg[:, g, :, :], in_=wst[:, g, :, :].rearrange("p t n -> p n t"))
+        for g in range(2):
+            nc.vector.quantize_mx(
+                out=wc[:, g, :].bitcast(FP8X4),
+                scales=ws[:, g, :],
+                in_=wg[:, g, :, :].rearrange("p n t -> p (n t)"),
+            )
+
+        a1 = const.tile([P, 32], F32, name="a1")
+        a_flat = a_bf[:].rearrange("p b c -> p (b c)")
+        nc.vector.tensor_scalar(out=a1[:], in0=a_flat, scalar1=-1.0, scalar2=1.0, op0=ALU.mult, op1=ALU.add)
+        nc.vector.tensor_tensor(out=a1[:], in0=a1[:], in1=a_flat, op=ALU.mult)
+        wgt = const.tile([P, 32], F32, name="wgt")
+        nc.gpsimd.tensor_tensor(out=wgt[:], in0=a1[:], in1=half_p[:], op=ALU.pow)
+
+        rv = rag_feat.rearrange("b k (i c) d -> b i k (c d)", c=4)
+        ov = orig_feat.rearrange("b (i c) d -> b i (c d)", c=4)
+        outv = out.rearrange("b (i c) d -> b i (c d)", c=4)
+
+        for b in range(NB):
+            for pi in range(2):
+                cols = slice(pi * 512, (pi + 1) * 512)
+                r = rpool.tile([P, NK, 512], BF16, name="r")
+                nc.sync.dma_start(out=r[:], in_=rv[b, :, :, cols])
+                o = rpool.tile([P, 512], BF16, name="o")
+                nc.sync.dma_start(out=o[:], in_=ov[b, :, cols])
+
+                m = work.tile([P, 4, 512], BF16, name="m", bufs=2)
+                nc.vector.tensor_tensor(out=m[:], in0=r[:, 0:4, :], in1=r[:, 4:8, :], op=ALU.max)
+                nc.vector.tensor_tensor(out=m[:, 0:2, :], in0=m[:, 0:2, :], in1=m[:, 2:4, :], op=ALU.max)
+                nc.vector.tensor_tensor(out=m[:, 0, :], in0=m[:, 0, :], in1=m[:, 1, :], op=ALU.max)
+
+                f = fpool.tile([P, NK + 1, 4, 2, 64], F32, name="f")
+                for hb in range(2):
+                    cl = 1 - hb
+                    tau = b * 4 + pi * 2 + cl
+                    fc = slice(cl * 256, (cl + 1) * 256)
+                    nc.vector.tensor_scalar(
+                        out=f[:, 0:KV, :, hb, :],
+                        in0=r[:, 0:KV, fc].rearrange("p k (j t) -> p k t j", t=4),
+                        scalar1=sc1[:, tau : tau + 1],
+                        scalar2=None,
+                        op0=ALU.mult,
+                    )
+                    nc.scalar.activation(
+                        out=f[:, KV:NK, :, hb, :],
+                        in_=r[:, KV:NK, fc].rearrange("p k (j t) -> p k t j", t=4),
+                        func=ACT.Copy,
+                        scale=sc1[:, tau : tau + 1],
+                    )
+                    nc.scalar.activation(
+                        out=f[:, NK, :, hb, :],
+                        in_=m[:, 0, fc].rearrange("p (j t) -> p t j", t=4),
+                        func=ACT.Copy,
+                        scale=sc2[:, tau : tau + 1],
+                    )
+
+                acc_ps = psum.tile([P, 4, 128], F32, tag="acc", bufs=2, name="acc_ps")
+                for t in range(4):
+                    for q in range(NK + 1):
+                        nc.tensor.matmul(
+                            acc_ps[:, t, :],
+                            lhsT=f[:, q, t, :, :].rearrange("p h j -> p (h j)"),
+                            rhs=ident_f[:],
+                            is_transpose=True,
+                            start=(q == 0),
+                            stop=(q == NK),
+                        )
+                o_ps = psum.tile([P, 2, 128], F32, tag="o", bufs=1, name="o_ps")
+                o_words = o[:].bitcast(F32).rearrange("p (j u) -> p u j", u=2)
+                for u in range(2):
+                    nc.tensor.transpose(o_ps[:, u, :], o_words[:, u, :], ident_f[:])
+
+                g = work.tile([P, 2, 128, 4], BF16, name="g", align_bytes=64)
+                nc.vector.tensor_copy(
+                    out=g[:, 0, :, :].bitcast(F32), in_=o_ps[:].rearrange("p u i -> p i u")
+                )
+                nc.scalar.copy(out=g[:, 1, :, :], in_=acc_ps[:].rearrange("p t i -> p i t"))
+                gc = work.tile([P, 256], U32, name="gc", align_bytes=64)
+                gs = work.tile([P, 256], U8, name="gs", align_bytes=64)
+                nc.vector.quantize_mx(
+                    out=gc[:].bitcast(FP8X4), scales=gs[:], in_=g[:].rearrange("p g i t -> p (g i t)")
+                )
+
+                y_ps = psum.tile([P, 2, 256], F32, tag="y", bufs=2, name="y_ps")
+                for gi in range(2):
+                    nc.tensor.matmul_mx(
+                        out=y_ps[:].rearrange("p h n -> p (h n)"),
+                        lhsT=gc[:, gi * 128 : (gi + 1) * 128].bitcast(FP8X4),
+                        lhsT_scale=gs[:, gi * 128 : (gi + 1) * 128],
+                        rhs=wc[:, gi, :].bitcast(FP8X4),
+                        rhs_scale=ws[:, gi, :],
+                        start=(gi == 0),
+                        stop=(gi == 1),
+                    )
+
+                yb = work.tile([P, 2, 256], F32, name="yb")
+                ysum = tiny.tile([P, 2], F32, name="ysum")
+                for hf in range(2):
+                    nc.vector.scalar_tensor_tensor(
+                        out=yb[:, hf, :],
+                        in0=y_ps[:, hf, :],
+                        scalar=1.0,
+                        in1=bias_bc[:],
+                        op0=ALU.mult,
+                        op1=ALU.add,
+                        accum_out=ysum[:, hf : hf + 1],
+                    )
+                negmu = tiny.tile([P, 2], F32, name="negmu")
+                nc.gpsimd.tensor_scalar(
+                    out=negmu[:], in0=ysum[:], scalar1=-1.0 / 256.0, scalar2=0.0, op0=ALU.mult, op1=ALU.add
+                )
+                junk = work.tile([P, 256], BF16, name="junk", bufs=2)
+                ssq = tiny.tile([P, 2], F32, name="ssq")
+                for hf in range(2):
+                    nc.scalar.activation(
+                        out=junk[:],
+                        in_=yb[:, hf, :],
+                        func=ACT.Square,
+                        bias=negmu[:, hf : hf + 1],
+                        accum_out=ssq[:, hf : hf + 1],
+                    )
+                ve = tiny.tile([P, 2], F32, name="ve")
+                nc.gpsimd.tensor_scalar(
+                    out=ve[:], in0=ssq[:], scalar1=1.0 / 256.0, scalar2=1e-5, op0=ALU.mult, op1=ALU.add
+                )
+                rstd = tiny.tile([P, 2], F32, name="rstd")
+                nc.gpsimd.tensor_tensor(out=rstd[:], in0=ve[:], in1=half_n[:], op=ALU.pow)
+                nmr = tiny.tile([P, 2], F32, name="nmr")
+                nc.gpsimd.tensor_tensor(out=nmr[:], in0=negmu[:], in1=rstd[:], op=ALU.mult)
+                z = work.tile([P, 2, 256], F32, name="z")
+                for hf in range(2):
+                    nc.scalar.activation(
+                        out=z[:, hf, :],
+                        in_=yb[:, hf, :],
+                        func=ACT.Identity,
+                        scale=rstd[:, hf : hf + 1],
+                        bias=nmr[:, hf : hf + 1],
+                    )
+                zt_ps = psum.tile([P, 2, 2, 128], F32, tag="zt", bufs=1, name="zt_ps")
+                for dh in range(2):
+                    for hf in range(2):
+                        nc.tensor.transpose(
+                            zt_ps[:, dh, hf, :], z[:, hf, dh * 128 : (dh + 1) * 128], ident_f[:]
+                        )
+                get = work.tile([P, 2, 2, 128], F32, name="get", bufs=2)
+                for dh in range(2):
+                    nc.scalar.activation(
+                        out=get[:, dh, :, :],
+                        in_=zt_ps[:, dh, :, :],
+                        func=ACT.Gelu,
+                        scale=vcol[:, 2 + dh : 3 + dh],
+                        bias=vcol[:, 4 + dh : 5 + dh],
+                    )
+                f_ps = psum.tile([P, 2, 2, 128], F32, tag="f", bufs=2, name="f_ps")
+                for hf in range(2):
+                    for dh in range(2):
+                        nc.tensor.transpose(f_ps[:, hf, dh, :], get[:, dh, hf, :], ident_f[:])
+                res = work.tile([P, 2, 256], F32, name="res")
+                for hf in range(2):
+                    tau = b * 4 + pi * 2 + hf
+                    nc.vector.scalar_tensor_tensor(
+                        out=res[:, hf, :],
+                        in0=f_ps[:, hf, :, :].rearrange("p a d -> p (a d)"),
+                        scalar=wgt[:, tau : tau + 1],
+                        in1=o[:, hf * 256 : (hf + 1) * 256],
+                        op0=ALU.mult,
+                        op1=ALU.add,
+                    )
+                nc.sync.dma_start(out=outv[b, :, cols], in_=res[:].rearrange("p h d -> p (h d)"))

@@ -17,7 +17,9 @@ P = 128
 NB = 8
 NK = 8
 D = 256
+NPAIR = 16
 KV = 5
+AHEAD = 2
 
 
 def tile_rarevariantawarefusion_pa_t_kernel(
@@ -27,17 +29,35 @@ def tile_rarevariantawarefusion_pa_t_kernel(
     with ExitStack() as ctx:
         const = ctx.enter_context(tc.tile_pool(name="const", bufs=1))
         s1 = ctx.enter_context(tc.tile_pool(name="s1", bufs=2))
-        rpool = ctx.enter_context(tc.tile_pool(name="rpool", bufs=5))
+        rpool = ctx.enter_context(tc.tile_pool(name="rpool", bufs=4))
+        opool = ctx.enter_context(tc.tile_pool(name="opool", bufs=10))
         fpool = ctx.enter_context(tc.tile_pool(name="fpool", bufs=3))
         work = ctx.enter_context(tc.tile_pool(name="work", bufs=3))
         tiny = ctx.enter_context(tc.tile_pool(name="tiny", bufs=4))
         psum = ctx.enter_context(tc.psum_pool(name="psum", bufs=1))
+        ctx.enter_context(tc.manual_schedule())
+
+        rv = rag_feat.rearrange("b k (i c) d -> b i k (c d)", c=4)
+        ov = orig_feat.rearrange("b (i c) d -> b i (c d)", c=4)
+        outv = out.rearrange("b (i c) d -> b i (c d)", c=4)
+        tl = {}
+
+        def load(n):
+            cols = slice((n % 2) * 512, (n % 2 + 1) * 512)
+            r = rpool.tile([P, NK, 512], BF16, name="r")
+            nc.sync.dma_start(out=r[:], in_=rv[n // 2, :, :, cols])
+            o = opool.tile([P, 512], BF16, name="o")
+            nc.sync.dma_start(out=o[:], in_=ov[n // 2, :, cols])
+            tl["r", n] = r
+            tl["o", n] = o
 
         h_sb = const.tile([P, NB, 4, 128], BF16, name="h_sb")
         nc.sync.dma_start(
             out=h_sb[:].rearrange("p b c h -> p b (c h)"),
             in_=h_af.rearrange("b (i c) h -> i b (c h)", c=4),
         )
+        for n in range(AHEAD):
+            load(n)
         w2_sb = const.tile([P, D], BF16, name="w2_sb")
         nc.scalar.dma_start(out=w2_sb[:], in_=w2)
         vrow = const.tile([P, P], BF16, name="vrow")
@@ -45,20 +65,7 @@ def tile_rarevariantawarefusion_pa_t_kernel(
         nc.scalar.dma_start(out=vrow[0:2, :], in_=b2.rearrange("(r c) -> r c", r=2))
         nc.scalar.dma_start(out=vrow[2:4, :], in_=ln_g.rearrange("(r c) -> r c", r=2))
         nc.scalar.dma_start(out=vrow[4:6, :], in_=ln_b.rearrange("(r c) -> r c", r=2))
-
-        ident_b = const.tile([P, P], BF16, name="ident_b")
-        make_identity(nc, ident_b[:])
-        ident_f = const.tile([P, P], F32, name="ident_f")
-        make_identity(nc, ident_f[:])
-        ones_f = const.tile([P, 2], F32, name="ones_f")
-        nc.vector.memset(ones_f[:], 1.0)
-        half_p = const.tile([P, 32], F32, name="half_p")
-        nc.vector.memset(half_p[:], 0.5)
-        half_n = const.tile([P, 2], F32, name="half_n")
-        nc.vector.memset(half_n[:], -0.5)
-
         wst = const.tile([P, 2, 4, 512], BF16, name="wst")
-        nc.vector.memset(wst[:], 0.0)
         top = wf[0:256, :].rearrange("(j t) n -> j t n", t=4)
         bot = wf[256:512, :].rearrange("(j t) n -> j t n", t=4)
         nc.scalar.dma_start(out=wst[0:64, 0, :, 0:256], in_=top)
@@ -70,57 +77,290 @@ def tile_rarevariantawarefusion_pa_t_kernel(
         a_bf = const.tile([P, NB, 4], BF16, name="a_bf")
         nc.scalar.dma_start(out=a_bf[:], in_=af.rearrange("b (i c) -> i b c", c=4))
 
+        ident_b = const.tile([P, P], BF16, name="ident_b")
+        make_identity(nc, ident_b[:])
+        ident_f = const.tile([P, P], F32, name="ident_f")
+        make_identity(nc, ident_f[:])
+        nc.gpsimd.memset(wst[64:128, 0, :, 0:256], 0.0)
+        nc.gpsimd.memset(wst[0:64, 0, :, 256:512], 0.0)
+        nc.gpsimd.memset(wst[64:128, 1, :, 256:512], 0.0)
+        nc.gpsimd.memset(wst[0:64, 1, :, 0:256], 0.0)
+        ones_f = const.tile([P, 2], F32, name="ones_f")
+        nc.vector.memset(ones_f[:], 1.0)
+        half_p = const.tile([P, 32], F32, name="half_p")
+        nc.vector.memset(half_p[:], 0.5)
+        half_n = const.tile([P, 2], F32, name="half_n")
+        nc.vector.memset(half_n[:], -0.5)
+
         vt_ps = psum.tile([P, P], BF16, tag="f", bufs=2, name="vt_ps")
         nc.tensor.transpose(vt_ps[:], vrow[:], ident_b[:])
         vcol = const.tile([P, 8], F32, name="vcol")
         nc.vector.tensor_copy(out=vcol[:, 0:6], in_=vt_ps[:, 0:6])
 
-        sc1 = const.tile([P, 32], F32, name="sc1")
-        sc2 = const.tile([P, 32], F32, name="sc2")
-        for b in range(NB):
-            ht_ps = psum.tile([P, 4, 128], BF16, tag="o", bufs=1, name="ht_ps")
-            for c in range(4):
-                nc.tensor.transpose(ht_ps[:, c, :], h_sb[:, b, c, :], ident_b[:])
-            ht = s1.tile([P, 512], BF16, name="ht")
-            nc.vector.tensor_copy(out=ht[:], in_=ht_ps[:].rearrange("p c i -> p (c i)"))
-            sig = s1.tile([P, 2, 512], F32, name="sig")
-            for dh in range(2):
-                z_ps = psum.tile([P, 512], F32, tag="acc", bufs=2, name="z_ps")
-                nc.tensor.matmul(
-                    z_ps[:], lhsT=w2_sb[:, dh * 128 : (dh + 1) * 128], rhs=ht[:], start=True, stop=True
-                )
-                nc.scalar.activation(
-                    out=sig[:, dh, :], in_=z_ps[:], func=ACT.Sigmoid, bias=vcol[:, dh : dh + 1]
-                )
-            s_ps = psum.tile([P, 4], F32, tag="zt", bufs=1, name="s_ps")
-            for c in range(4):
-                for dh in range(2):
-                    nc.tensor.matmul(
-                        s_ps[:, c : c + 1],
-                        lhsT=sig[:, dh, c * 128 : (c + 1) * 128],
-                        rhs=ones_f[:, 0:1],
-                        start=(dh == 0),
-                        stop=(dh == 1),
-                    )
-            nc.vector.tensor_scalar(
-                out=sc1[:, b * 4 : (b + 1) * 4], in0=s_ps[:], scalar1=0.7 / 8.0, scalar2=None, op0=ALU.mult
-            )
-            nc.vector.tensor_scalar(
-                out=sc2[:, b * 4 : (b + 1) * 4], in0=s_ps[:], scalar1=0.3, scalar2=None, op0=ALU.mult
-            )
-
         wg = const.tile([P, 2, 512, 4], BF16, name="wg", align_bytes=64)
         wc = const.tile([P, 2, 512], U32, name="wc", align_bytes=64)
         ws = const.tile([P, 2, 512], U8, name="ws", align_bytes=64)
-        for g in range(2):
-            nc.vector.tensor_copy(out=wg[:, g, :, :], in_=wst[:, g, :, :].rearrange("p t n -> p n t"))
-        for g in range(2):
-            nc.vector.quantize_mx(
-                out=wc[:, g, :].bitcast(FP8X4),
-                scales=ws[:, g, :],
-                in_=wg[:, g, :, :].rearrange("p n t -> p (n t)"),
+        for gi in range(2):
+            nc.gpsimd.tensor_scalar(
+                out=wg[:, gi, :, :],
+                in0=wst[:, gi, :, :].rearrange("p t n -> p n t"),
+                scalar1=1.0,
+                scalar2=0.0,
+                op0=ALU.mult,
+                op1=ALU.add,
             )
 
+        sc1 = const.tile([P, 32], F32, name="sc1")
+        sc2 = const.tile([P, 32], F32, name="sc2")
+
+        def gate_step(j):
+            if j < NB:
+                ht_ps = psum.tile([P, 4, 128], BF16, tag="f", bufs=2, name="ht_ps")
+                for c in range(4):
+                    nc.tensor.transpose(ht_ps[:, c, :], h_sb[:, j, c, :], ident_b[:])
+                ht = s1.tile([P, 512], BF16, name="ht")
+                nc.vector.tensor_copy(out=ht[:], in_=ht_ps[:].rearrange("p c i -> p (c i)"))
+                tl["ht", j] = ht
+            if 0 <= j - 1 < NB:
+                sig = s1.tile([P, 2, 512], F32, name="sig")
+                for dh in range(2):
+                    z_ps = psum.tile([P, 512], F32, tag=("z1", "zt")[dh], bufs=1, name="z_ps")
+                    nc.tensor.matmul(
+                        z_ps[:],
+                        lhsT=w2_sb[:, dh * 128 : (dh + 1) * 128],
+                        rhs=tl["ht", j - 1][:],
+                        start=True,
+                        stop=True,
+                    )
+                    nc.scalar.activation(
+                        out=sig[:, dh, :], in_=z_ps[:], func=ACT.Sigmoid, bias=vcol[:, dh : dh + 1]
+                    )
+                tl["sig", j - 1] = sig
+            if 0 <= j - 2 < NB:
+                b = j - 2
+                sig = tl["sig", b]
+                s_ps = psum.tile([P, 4], F32, tag="f", bufs=2, name="s_ps")
+                for c in range(4):
+                    for dh in range(2):
+                        nc.tensor.matmul(
+                            s_ps[:, c : c + 1],
+                            lhsT=sig[:, dh, c * 128 : (c + 1) * 128],
+                            rhs=ones_f[:, 0:1],
+                            start=(dh == 0),
+                            stop=(dh == 1),
+                        )
+                nc.vector.tensor_scalar(
+                    out=sc1[:, b * 4 : (b + 1) * 4], in0=s_ps[:], scalar1=0.7 / 8.0, scalar2=None, op0=ALU.mult
+                )
+                nc.vector.tensor_scalar(
+                    out=sc2[:, b * 4 : (b + 1) * 4], in0=s_ps[:], scalar1=0.3, scalar2=None, op0=ALU.mult
+                )
+
+        def planes_scalar(n):
+            f = fpool.tile([P, NK + 1, 4, 2, 64], F32, name="f")
+            tl["f", n] = f
+            r = tl["r", n]
+            for hb in range(2):
+                cl = 1 - hb
+                tau = n * 2 + cl
+                nc.scalar.activation(
+                    out=f[:, KV:NK, :, hb, :],
+                    in_=r[:, KV:NK, cl * 256 : (cl + 1) * 256].rearrange("p k (j t) -> p k t j", t=4),
+                    func=ACT.Copy,
+                    scale=sc1[:, tau : tau + 1],
+                )
+
+        def max_and_planes_vector(n):
+            r = tl["r", n]
+            f = tl["f", n]
+            m = work.tile([P, 4, 512], BF16, name="m", bufs=2)
+            tl["m", n] = m
+            nc.vector.tensor_tensor(out=m[:], in0=r[:, 0:4, :], in1=r[:, 4:8, :], op=ALU.max)
+            nc.vector.tensor_tensor(out=m[:, 0:2, :], in0=m[:, 0:2, :], in1=m[:, 2:4, :], op=ALU.max)
+            nc.vector.tensor_tensor(out=m[:, 0, :], in0=m[:, 0, :], in1=m[:, 1, :], op=ALU.max)
+            for hb in range(2):
+                cl = 1 - hb
+                tau = n * 2 + cl
+                nc.vector.tensor_scalar(
+                    out=f[:, 0:KV, :, hb, :],
+                    in0=r[:, 0:KV, cl * 256 : (cl + 1) * 256].rearrange("p k (j t) -> p k t j", t=4),
+                    scalar1=sc1[:, tau : tau + 1],
+                    scalar2=None,
+                    op0=ALU.mult,
+                )
+
+        def max_plane_scalar(n):
+            f = tl["f", n]
+            m = tl["m", n]
+            for hb in range(2):
+                cl = 1 - hb
+                tau = n * 2 + cl
+                nc.scalar.activation(
+                    out=f[:, NK, :, hb, :],
+                    in_=m[:, 0, cl * 256 : (cl + 1) * 256].rearrange("p (j t) -> p t j", t=4),
+                    func=ACT.Copy,
+                    scale=sc2[:, tau : tau + 1],
+                )
+
+        def add_up(n):
+            f = tl["f", n]
+            acc_ps = psum.tile([P, 4, 128], F32, tag="acc", bufs=2, name="acc_ps")
+            tl["acc", n] = acc_ps
+            for t in range(4):
+                for q in range(NK + 1):
+                    nc.tensor.matmul(
+                        acc_ps[:, t, :],
+                        lhsT=f[:, q, t, :, :].rearrange("p h j -> p (h j)"),
+                        rhs=ident_f[:],
+                        is_transpose=True,
+                        start=(q == 0),
+                        stop=(q == NK),
+                    )
+            o_ps = psum.tile([P, 2, 128], F32, tag="o", bufs=1, name="o_ps")
+            tl["o_ps", n] = o_ps
+            o_words = tl["o", n][:].bitcast(F32).rearrange("p (j u) -> p u j", u=2)
+            for u in range(2):
+                nc.tensor.transpose(o_ps[:, u, :], o_words[:, u, :], ident_f[:])
+
+        def leave_psum(n):
+            g = work.tile([P, 2, 128, 4], BF16, name="g", align_bytes=64)
+            tl["g", n] = g
+            nc.scalar.copy(out=g[:, 1, :, :], in_=tl["acc", n][:].rearrange("p t i -> p i t"))
+            nc.vector.tensor_copy(
+                out=g[:, 0, :, :].bitcast(F32), in_=tl["o_ps", n][:].rearrange("p u i -> p i u")
+            )
+
+        def quantise(n):
+            gc = work.tile([P, 256], U32, name="gc", align_bytes=64)
+            gs = work.tile([P, 256], U8, name="gs", align_bytes=64)
+            tl["gc", n] = gc
+            tl["gs", n] = gs
+            nc.vector.quantize_mx(
+                out=gc[:].bitcast(FP8X4), scales=gs[:], in_=tl["g", n][:].rearrange("p g i t -> p (g i t)")
+            )
+
+        def multiply(n):
+            gc = tl["gc", n]
+            gs = tl["gs", n]
+            y_ps = psum.tile([P, 2, 256], F32, tag="y", bufs=1, name="y_ps")
+            tl["y", n] = y_ps
+            for gi in range(2):
+                nc.tensor.matmul_mx(
+                    out=y_ps[:].rearrange("p h n -> p (h n)"),
+                    lhsT=gc[:, gi * 128 : (gi + 1) * 128].bitcast(FP8X4),
+                    lhsT_scale=gs[:, gi * 128 : (gi + 1) * 128],
+                    rhs=wc[:, gi, :].bitcast(FP8X4),
+                    rhs_scale=ws[:, gi, :],
+                    start=(gi == 0),
+                    stop=(gi == 1),
+                )
+
+        def bias_and_mean(n):
+            y_ps = tl["y", n]
+            yb = work.tile([P, 2, 256], F32, name="yb")
+            ysum = tiny.tile([P, 2], F32, name="ysum")
+            tl["yb", n] = yb
+            for hf in range(2):
+                nc.vector.scalar_tensor_tensor(
+                    out=yb[:, hf, :],
+                    in0=y_ps[:, hf, :],
+                    scalar=1.0,
+                    in1=bias_bc[:],
+                    op0=ALU.mult,
+                    op1=ALU.add,
+                    accum_out=ysum[:, hf : hf + 1],
+                )
+            negmu = tiny.tile([P, 2], F32, name="negmu")
+            tl["negmu", n] = negmu
+            nc.vector.tensor_scalar(
+                out=negmu[:], in0=ysum[:], scalar1=-1.0 / 256.0, scalar2=None, op0=ALU.mult
+            )
+
+        def variance(n):
+            yb = tl["yb", n]
+            negmu = tl["negmu", n]
+            junk = work.tile([P, 256], BF16, name="junk", bufs=2)
+            ssq = tiny.tile([P, 2], F32, name="ssq")
+            for hf in range(2):
+                nc.scalar.activation(
+                    out=junk[:],
+                    in_=yb[:, hf, :],
+                    func=ACT.Square,
+                    bias=negmu[:, hf : hf + 1],
+                    accum_out=ssq[:, hf : hf + 1],
+                )
+            ve = tiny.tile([P, 2], F32, name="ve")
+            nc.gpsimd.tensor_scalar(
+                out=ve[:], in0=ssq[:], scalar1=1.0 / 256.0, scalar2=1e-5, op0=ALU.mult, op1=ALU.add
+            )
+            rstd = tiny.tile([P, 2], F32, name="rstd")
+            nc.gpsimd.tensor_tensor(out=rstd[:], in0=ve[:], in1=half_n[:], op=ALU.pow)
+            nmr = tiny.tile([P, 2], F32, name="nmr")
+            nc.gpsimd.tensor_tensor(out=nmr[:], in0=negmu[:], in1=rstd[:], op=ALU.mult)
+            tl["rstd", n] = rstd
+            tl["nmr", n] = nmr
+
+        def normalise(n):
+            yb = tl["yb", n]
+            z = work.tile([P, 2, 256], F32, name="z", bufs=2)
+            tl["z", n] = z
+            for hf in range(2):
+                nc.scalar.activation(
+                    out=z[:, hf, :],
+                    in_=yb[:, hf, :],
+                    func=ACT.Identity,
+                    scale=tl["rstd", n][:, hf : hf + 1],
+                    bias=tl["nmr", n][:, hf : hf + 1],
+                )
+
+        def turn(n):
+            z = tl["z", n]
+            zt_ps = psum.tile([P, 2, 2, 128], F32, tag="zt", bufs=1, name="zt_ps")
+            tl["zt", n] = zt_ps
+            for dh in range(2):
+                for hf in range(2):
+                    nc.tensor.transpose(zt_ps[:, dh, hf, :], z[:, hf, dh * 128 : (dh + 1) * 128], ident_f[:])
+
+        def gelu(n):
+            get = work.tile([P, 2, 2, 128], F32, name="get", bufs=2)
+            tl["get", n] = get
+            for dh in range(2):
+                nc.scalar.activation(
+                    out=get[:, dh, :, :],
+                    in_=tl["zt", n][:, dh, :, :],
+                    func=ACT.Gelu,
+                    scale=vcol[:, 2 + dh : 3 + dh],
+                    bias=vcol[:, 4 + dh : 5 + dh],
+                )
+
+        def turn_back(n):
+            get = tl["get", n]
+            f_ps = psum.tile([P, 2, 2, 128], F32, tag="f", bufs=2, name="f_ps")
+            tl["f_ps", n] = f_ps
+            for hf in range(2):
+                for dh in range(2):
+                    nc.tensor.transpose(f_ps[:, hf, dh, :], get[:, dh, hf, :], ident_f[:])
+
+        def residual_and_store(n):
+            res = work.tile([P, 2, 256], F32, name="res")
+            for hf in range(2):
+                tau = n * 2 + hf
+                nc.vector.scalar_tensor_tensor(
+                    out=res[:, hf, :],
+                    in0=tl["f_ps", n][:, hf, :, :].rearrange("p a d -> p (a d)"),
+                    scalar=wgt[:, tau : tau + 1],
+                    in1=tl["o", n][:, hf * 256 : (hf + 1) * 256],
+                    op0=ALU.mult,
+                    op1=ALU.add,
+                )
+            cols = slice((n % 2) * 512, (n % 2 + 1) * 512)
+            nc.sync.dma_start(out=outv[n // 2, :, cols], in_=res[:].rearrange("p h d -> p (h d)"))
+
+        def on(n):
+            return 0 <= n < NPAIR
+
+        for j in range(3):
+            gate_step(j)
         a1 = const.tile([P, 32], F32, name="a1")
         a_flat = a_bf[:].rearrange("p b c -> p (b c)")
         nc.vector.tensor_scalar(out=a1[:], in0=a_flat, scalar1=-1.0, scalar2=1.0, op0=ALU.mult, op1=ALU.add)
@@ -128,158 +368,43 @@ def tile_rarevariantawarefusion_pa_t_kernel(
         wgt = const.tile([P, 32], F32, name="wgt")
         nc.gpsimd.tensor_tensor(out=wgt[:], in0=a1[:], in1=half_p[:], op=ALU.pow)
 
-        rv = rag_feat.rearrange("b k (i c) d -> b i k (c d)", c=4)
-        ov = orig_feat.rearrange("b (i c) d -> b i (c d)", c=4)
-        outv = out.rearrange("b (i c) d -> b i (c d)", c=4)
-
-        for b in range(NB):
-            for pi in range(2):
-                cols = slice(pi * 512, (pi + 1) * 512)
-                r = rpool.tile([P, NK, 512], BF16, name="r")
-                nc.sync.dma_start(out=r[:], in_=rv[b, :, :, cols])
-                o = rpool.tile([P, 512], BF16, name="o")
-                nc.sync.dma_start(out=o[:], in_=ov[b, :, cols])
-
-                m = work.tile([P, 4, 512], BF16, name="m", bufs=2)
-                nc.vector.tensor_tensor(out=m[:], in0=r[:, 0:4, :], in1=r[:, 4:8, :], op=ALU.max)
-                nc.vector.tensor_tensor(out=m[:, 0:2, :], in0=m[:, 0:2, :], in1=m[:, 2:4, :], op=ALU.max)
-                nc.vector.tensor_tensor(out=m[:, 0, :], in0=m[:, 0, :], in1=m[:, 1, :], op=ALU.max)
-
-                f = fpool.tile([P, NK + 1, 4, 2, 64], F32, name="f")
-                for hb in range(2):
-                    cl = 1 - hb
-                    tau = b * 4 + pi * 2 + cl
-                    fc = slice(cl * 256, (cl + 1) * 256)
-                    nc.vector.tensor_scalar(
-                        out=f[:, 0:KV, :, hb, :],
-                        in0=r[:, 0:KV, fc].rearrange("p k (j t) -> p k t j", t=4),
-                        scalar1=sc1[:, tau : tau + 1],
-                        scalar2=None,
-                        op0=ALU.mult,
-                    )
-                    nc.scalar.activation(
-                        out=f[:, KV:NK, :, hb, :],
-                        in_=r[:, KV:NK, fc].rearrange("p k (j t) -> p k t j", t=4),
-                        func=ACT.Copy,
-                        scale=sc1[:, tau : tau + 1],
-                    )
-                    nc.scalar.activation(
-                        out=f[:, NK, :, hb, :],
-                        in_=m[:, 0, fc].rearrange("p (j t) -> p t j", t=4),
-                        func=ACT.Copy,
-                        scale=sc2[:, tau : tau + 1],
-                    )
-
-                acc_ps = psum.tile([P, 4, 128], F32, tag="acc", bufs=2, name="acc_ps")
-                for t in range(4):
-                    for q in range(NK + 1):
-                        nc.tensor.matmul(
-                            acc_ps[:, t, :],
-                            lhsT=f[:, q, t, :, :].rearrange("p h j -> p (h j)"),
-                            rhs=ident_f[:],
-                            is_transpose=True,
-                            start=(q == 0),
-                            stop=(q == NK),
-                        )
-                o_ps = psum.tile([P, 2, 128], F32, tag="o", bufs=1, name="o_ps")
-                o_words = o[:].bitcast(F32).rearrange("p (j u) -> p u j", u=2)
-                for u in range(2):
-                    nc.tensor.transpose(o_ps[:, u, :], o_words[:, u, :], ident_f[:])
-
-                g = work.tile([P, 2, 128, 4], BF16, name="g", align_bytes=64)
-                nc.vector.tensor_copy(
-                    out=g[:, 0, :, :].bitcast(F32), in_=o_ps[:].rearrange("p u i -> p i u")
-                )
-                nc.scalar.copy(out=g[:, 1, :, :], in_=acc_ps[:].rearrange("p t i -> p i t"))
-                gc = work.tile([P, 256], U32, name="gc", align_bytes=64)
-                gs = work.tile([P, 256], U8, name="gs", align_bytes=64)
-                nc.vector.quantize_mx(
-                    out=gc[:].bitcast(FP8X4), scales=gs[:], in_=g[:].rearrange("p g i t -> p (g i t)")
-                )
-
-                y_ps = psum.tile([P, 2, 256], F32, tag="y", bufs=2, name="y_ps")
+        for n in range(NPAIR + 7):
+            if on(n + AHEAD):
+                load(n + AHEAD)
+            if on(n - 6):
+                turn_back(n - 6)
+            if on(n - 5):
+                turn(n - 5)
+            if on(n - 2):
+                leave_psum(n - 2)
+            if on(n - 3):
+                bias_and_mean(n - 3)
+            if on(n - 2):
+                quantise(n - 2)
+            if n == 1:
                 for gi in range(2):
-                    nc.tensor.matmul_mx(
-                        out=y_ps[:].rearrange("p h n -> p (h n)"),
-                        lhsT=gc[:, gi * 128 : (gi + 1) * 128].bitcast(FP8X4),
-                        lhsT_scale=gs[:, gi * 128 : (gi + 1) * 128],
-                        rhs=wc[:, gi, :].bitcast(FP8X4),
-                        rhs_scale=ws[:, gi, :],
-                        start=(gi == 0),
-                        stop=(gi == 1),
+                    nc.vector.quantize_mx(
+                        out=wc[:, gi, :].bitcast(FP8X4),
+                        scales=ws[:, gi, :],
+                        in_=wg[:, gi, :, :].rearrange("p n t -> p (n t)"),
                     )
-
-                yb = work.tile([P, 2, 256], F32, name="yb")
-                ysum = tiny.tile([P, 2], F32, name="ysum")
-                for hf in range(2):
-                    nc.vector.scalar_tensor_tensor(
-                        out=yb[:, hf, :],
-                        in0=y_ps[:, hf, :],
-                        scalar=1.0,
-                        in1=bias_bc[:],
-                        op0=ALU.mult,
-                        op1=ALU.add,
-                        accum_out=ysum[:, hf : hf + 1],
-                    )
-                negmu = tiny.tile([P, 2], F32, name="negmu")
-                nc.gpsimd.tensor_scalar(
-                    out=negmu[:], in0=ysum[:], scalar1=-1.0 / 256.0, scalar2=0.0, op0=ALU.mult, op1=ALU.add
-                )
-                junk = work.tile([P, 256], BF16, name="junk", bufs=2)
-                ssq = tiny.tile([P, 2], F32, name="ssq")
-                for hf in range(2):
-                    nc.scalar.activation(
-                        out=junk[:],
-                        in_=yb[:, hf, :],
-                        func=ACT.Square,
-                        bias=negmu[:, hf : hf + 1],
-                        accum_out=ssq[:, hf : hf + 1],
-                    )
-                ve = tiny.tile([P, 2], F32, name="ve")
-                nc.gpsimd.tensor_scalar(
-                    out=ve[:], in0=ssq[:], scalar1=1.0 / 256.0, scalar2=1e-5, op0=ALU.mult, op1=ALU.add
-                )
-                rstd = tiny.tile([P, 2], F32, name="rstd")
-                nc.gpsimd.tensor_tensor(out=rstd[:], in0=ve[:], in1=half_n[:], op=ALU.pow)
-                nmr = tiny.tile([P, 2], F32, name="nmr")
-                nc.gpsimd.tensor_tensor(out=nmr[:], in0=negmu[:], in1=rstd[:], op=ALU.mult)
-                z = work.tile([P, 2, 256], F32, name="z")
-                for hf in range(2):
-                    nc.scalar.activation(
-                        out=z[:, hf, :],
-                        in_=yb[:, hf, :],
-                        func=ACT.Identity,
-                        scale=rstd[:, hf : hf + 1],
-                        bias=nmr[:, hf : hf + 1],
-                    )
-                zt_ps = psum.tile([P, 2, 2, 128], F32, tag="zt", bufs=1, name="zt_ps")
-                for dh in range(2):
-                    for hf in range(2):
-                        nc.tensor.transpose(
-                            zt_ps[:, dh, hf, :], z[:, hf, dh * 128 : (dh + 1) * 128], ident_f[:]
-                        )
-                get = work.tile([P, 2, 2, 128], F32, name="get", bufs=2)
-                for dh in range(2):
-                    nc.scalar.activation(
-                        out=get[:, dh, :, :],
-                        in_=zt_ps[:, dh, :, :],
-                        func=ACT.Gelu,
-                        scale=vcol[:, 2 + dh : 3 + dh],
-                        bias=vcol[:, 4 + dh : 5 + dh],
-                    )
-                f_ps = psum.tile([P, 2, 2, 128], F32, tag="f", bufs=2, name="f_ps")
-                for hf in range(2):
-                    for dh in range(2):
-                        nc.tensor.transpose(f_ps[:, hf, dh, :], get[:, dh, hf, :], ident_f[:])
-                res = work.tile([P, 2, 256], F32, name="res")
-                for hf in range(2):
-                    tau = b * 4 + pi * 2 + hf
-                    nc.vector.scalar_tensor_tensor(
-                        out=res[:, hf, :],
-                        in0=f_ps[:, hf, :, :].rearrange("p a d -> p (a d)"),
-                        scalar=wgt[:, tau : tau + 1],
-                        in1=o[:, hf * 256 : (hf + 1) * 256],
-                        op0=ALU.mult,
-                        op1=ALU.add,
-                    )
-                nc.sync.dma_start(out=outv[b, :, cols], in_=res[:].rearrange("p h d -> p (h d)"))
+            if on(n - 1):
+                add_up(n - 1)
+            if on(n - 2):
+                multiply(n - 2)
+            if on(n):
+                planes_scalar(n)
+            if on(n - 5):
+                gelu(n - 5)
+            if on(n - 4):
+                normalise(n - 4)
+            if on(n - 3):
+                variance(n - 3)
+            if on(n):
+                max_and_planes_vector(n)
+                max_plane_scalar(n)
+            if n < 4:
+                gate_step(3 + 2 * n)
+                gate_step(4 + 2 * n)
+            if on(n - 6):
+                residual_and_store(n - 6)

@@ -202,11 +202,13 @@ def tile_rarevariantawarefusion_pa_t_kernel(
                     scale=sc2[:, tau : tau + 1],
                 )
 
-        def add_up(n):
+        def add_up(n, half):
             f = tl["f", n]
-            acc_ps = psum.tile([P, 4, 128], F32, tag="acc", bufs=2, name="acc_ps")
-            tl["acc", n] = acc_ps
-            for t in range(4):
+            if half == 0:
+                acc_ps = psum.tile([P, 4, 128], F32, tag="acc", bufs=2, name="acc_ps")
+                tl["acc", n] = acc_ps
+            acc_ps = tl["acc", n]
+            for t in range(2 * half, 2 * half + 2):
                 for q in range(NK + 1):
                     nc.tensor.matmul(
                         acc_ps[:, t, :],
@@ -216,6 +218,8 @@ def tile_rarevariantawarefusion_pa_t_kernel(
                         start=(q == 0),
                         stop=(q == NK),
                     )
+            if half == 0:
+                return
             o_ps = psum.tile([P, 2, 128], F32, tag="o", bufs=1, name="o_ps")
             tl["o_ps", n] = o_ps
             o_words = tl["o", n][:].bitcast(F32).rearrange("p (j u) -> p u j", u=2)
@@ -239,11 +243,24 @@ def tile_rarevariantawarefusion_pa_t_kernel(
                 out=gc[:].bitcast(FP8X4), scales=gs[:], in_=tl["g", n][:].rearrange("p g i t -> p (g i t)")
             )
 
+        def keep_clock(n):
+            y_ps = psum.tile([P, 2, 256], F32, tag="y", bufs=1, name="y_ps")
+            tl["y", n] = y_ps
+            for gi in range(2):
+                nc.tensor.matmul_mx(
+                    out=y_ps[:].rearrange("p h n -> p (h n)"),
+                    lhsT=wc[:, gi, 0:128].bitcast(FP8X4),
+                    lhsT_scale=ws[:, gi, 0:128],
+                    rhs=wc[:, gi, :].bitcast(FP8X4),
+                    rhs_scale=ws[:, gi, :],
+                    start=(gi == 0),
+                    stop=(gi == 1),
+                )
+
         def multiply(n):
             gc = tl["gc", n]
             gs = tl["gs", n]
-            y_ps = psum.tile([P, 2, 256], F32, tag="y", bufs=1, name="y_ps")
-            tl["y", n] = y_ps
+            y_ps = tl["y", n]
             for gi in range(2):
                 nc.tensor.matmul_mx(
                     out=y_ps[:].rearrange("p h n -> p (h n)"),
@@ -373,8 +390,6 @@ def tile_rarevariantawarefusion_pa_t_kernel(
                 load(n + AHEAD)
             if on(n - 6):
                 turn_back(n - 6)
-            if on(n - 5):
-                turn(n - 5)
             if on(n - 2):
                 leave_psum(n - 2)
             if on(n - 3):
@@ -389,15 +404,20 @@ def tile_rarevariantawarefusion_pa_t_kernel(
                         in_=wg[:, gi, :, :].rearrange("p n t -> p (n t)"),
                     )
             if on(n - 1):
-                add_up(n - 1)
+                add_up(n - 1, 0)
             if on(n - 2):
-                multiply(n - 2)
+                keep_clock(n - 2)
+            if on(n - 1):
+                add_up(n - 1, 1)
             if on(n):
                 planes_scalar(n)
             if on(n - 5):
                 gelu(n - 5)
             if on(n - 4):
                 normalise(n - 4)
+                turn(n - 4)
+            if on(n - 2):
+                multiply(n - 2)
             if on(n - 3):
                 variance(n - 3)
             if on(n):

@@ -18,8 +18,9 @@ NB = 8
 NK = 8
 D = 256
 NPAIR = 16
-KV = 5
+NQ = 4
 AHEAD = 2
+GATE_STEPS = {0: (3, 4), 1: (5, 6), 2: (7,), 3: (8,), 4: (9,)}
 
 
 def tile_rarevariantawarefusion_pa_t_kernel(
@@ -30,7 +31,7 @@ def tile_rarevariantawarefusion_pa_t_kernel(
         const = ctx.enter_context(tc.tile_pool(name="const", bufs=1))
         s1 = ctx.enter_context(tc.tile_pool(name="s1", bufs=2))
         rpool = ctx.enter_context(tc.tile_pool(name="rpool", bufs=4))
-        opool = ctx.enter_context(tc.tile_pool(name="opool", bufs=10))
+        opool = ctx.enter_context(tc.tile_pool(name="opool", bufs=11))
         fpool = ctx.enter_context(tc.tile_pool(name="fpool", bufs=3))
         work = ctx.enter_context(tc.tile_pool(name="work", bufs=3))
         tiny = ctx.enter_context(tc.tile_pool(name="tiny", bufs=4))
@@ -51,12 +52,13 @@ def tile_rarevariantawarefusion_pa_t_kernel(
             tl["r", n] = r
             tl["o", n] = o
 
+        load(0)
         h_sb = const.tile([P, NB, 4, 128], BF16, name="h_sb")
         nc.sync.dma_start(
             out=h_sb[:].rearrange("p b c h -> p b (c h)"),
             in_=h_af.rearrange("b (i c) h -> i b (c h)", c=4),
         )
-        for n in range(AHEAD):
+        for n in range(1, AHEAD):
             load(n)
         w2_sb = const.tile([P, D], BF16, name="w2_sb")
         nc.scalar.dma_start(out=w2_sb[:], in_=w2)
@@ -156,70 +158,63 @@ def tile_rarevariantawarefusion_pa_t_kernel(
                     out=sc2[:, b * 4 : (b + 1) * 4], in0=s_ps[:], scalar1=0.3, scalar2=None, op0=ALU.mult
                 )
 
-        def planes_scalar(n):
-            f = fpool.tile([P, NK + 1, 4, 2, 64], F32, name="f")
-            tl["f", n] = f
+        def max_and_sums(n):
             r = tl["r", n]
-            for hb in range(2):
-                cl = 1 - hb
-                tau = n * 2 + cl
-                nc.scalar.activation(
-                    out=f[:, KV:NK, :, hb, :],
-                    in_=r[:, KV:NK, cl * 256 : (cl + 1) * 256].rearrange("p k (j t) -> p k t j", t=4),
-                    func=ACT.Copy,
-                    scale=sc1[:, tau : tau + 1],
-                )
-
-        def max_and_planes_vector(n):
-            r = tl["r", n]
-            f = tl["f", n]
             m = work.tile([P, 4, 512], BF16, name="m", bufs=2)
+            qs = fpool.tile([P, NQ, 2, 4, 64], F32, name="qs")
             tl["m", n] = m
-            nc.vector.tensor_tensor(out=m[:], in0=r[:, 0:4, :], in1=r[:, 4:8, :], op=ALU.max)
-            nc.vector.tensor_tensor(out=m[:, 0:2, :], in0=m[:, 0:2, :], in1=m[:, 2:4, :], op=ALU.max)
-            nc.vector.tensor_tensor(out=m[:, 0, :], in0=m[:, 0, :], in1=m[:, 1, :], op=ALU.max)
-            for hb in range(2):
-                cl = 1 - hb
-                tau = n * 2 + cl
-                nc.vector.tensor_scalar(
-                    out=f[:, 0:KV, :, hb, :],
-                    in0=r[:, 0:KV, cl * 256 : (cl + 1) * 256].rearrange("p k (j t) -> p k t j", t=4),
-                    scalar1=sc1[:, tau : tau + 1],
-                    scalar2=None,
-                    op0=ALU.mult,
+            tl["qs", n] = qs
+
+            def pair_sums(cl):
+                fc = slice(cl * 256, (cl + 1) * 256)
+                nc.vector.tensor_tensor(
+                    out=qs[:, :, cl, :, :],
+                    in0=r[:, 0:4, fc].rearrange("p k (j t) -> p k t j", t=4),
+                    in1=r[:, 4:8, fc].rearrange("p k (j t) -> p k t j", t=4),
+                    op=ALU.add,
                 )
 
-        def max_plane_scalar(n):
-            f = tl["f", n]
+            nc.vector.tensor_tensor(out=m[:], in0=r[:, 0:4, :], in1=r[:, 4:8, :], op=ALU.max)
+            pair_sums(0)
+            nc.vector.tensor_tensor(out=m[:, 0:2, :], in0=m[:, 0:2, :], in1=m[:, 2:4, :], op=ALU.max)
+            pair_sums(1)
+            nc.vector.tensor_tensor(out=m[:, 0, :], in0=m[:, 0, :], in1=m[:, 1, :], op=ALU.max)
+
+        def planes(n):
+            f = fpool.tile([P, NQ + 1, 4, 2, 64], F32, name="f")
+            tl["f", n] = f
+            qs = tl["qs", n]
             m = tl["m", n]
             for hb in range(2):
                 cl = 1 - hb
                 tau = n * 2 + cl
                 nc.scalar.activation(
-                    out=f[:, NK, :, hb, :],
+                    out=f[:, 0:NQ, :, hb, :], in_=qs[:, :, cl, :, :], func=ACT.Copy, scale=sc1[:, tau : tau + 1]
+                )
+            for hb in range(2):
+                cl = 1 - hb
+                tau = n * 2 + cl
+                nc.scalar.activation(
+                    out=f[:, NQ, :, hb, :],
                     in_=m[:, 0, cl * 256 : (cl + 1) * 256].rearrange("p (j t) -> p t j", t=4),
                     func=ACT.Copy,
                     scale=sc2[:, tau : tau + 1],
                 )
 
-        def add_up(n, half):
+        def add_up(n):
             f = tl["f", n]
-            if half == 0:
-                acc_ps = psum.tile([P, 4, 128], F32, tag="acc", bufs=2, name="acc_ps")
-                tl["acc", n] = acc_ps
-            acc_ps = tl["acc", n]
-            for t in range(2 * half, 2 * half + 2):
-                for q in range(NK + 1):
+            acc_ps = psum.tile([P, 4, 128], F32, tag="acc", bufs=2, name="acc_ps")
+            tl["acc", n] = acc_ps
+            for t in range(4):
+                for q in range(NQ + 1):
                     nc.tensor.matmul(
                         acc_ps[:, t, :],
                         lhsT=f[:, q, t, :, :].rearrange("p h j -> p (h j)"),
                         rhs=ident_f[:],
                         is_transpose=True,
                         start=(q == 0),
-                        stop=(q == NK),
+                        stop=(q == NQ),
                     )
-            if half == 0:
-                return
             o_ps = psum.tile([P, 2, 128], F32, tag="o", bufs=1, name="o_ps")
             tl["o_ps", n] = o_ps
             o_words = tl["o", n][:].bitcast(F32).rearrange("p (j u) -> p u j", u=2)
@@ -243,24 +238,11 @@ def tile_rarevariantawarefusion_pa_t_kernel(
                 out=gc[:].bitcast(FP8X4), scales=gs[:], in_=tl["g", n][:].rearrange("p g i t -> p (g i t)")
             )
 
-        def keep_clock(n):
-            y_ps = psum.tile([P, 2, 256], F32, tag="y", bufs=1, name="y_ps")
-            tl["y", n] = y_ps
-            for gi in range(2):
-                nc.tensor.matmul_mx(
-                    out=y_ps[:].rearrange("p h n -> p (h n)"),
-                    lhsT=wc[:, gi, 0:128].bitcast(FP8X4),
-                    lhsT_scale=ws[:, gi, 0:128],
-                    rhs=wc[:, gi, :].bitcast(FP8X4),
-                    rhs_scale=ws[:, gi, :],
-                    start=(gi == 0),
-                    stop=(gi == 1),
-                )
-
         def multiply(n):
             gc = tl["gc", n]
             gs = tl["gs", n]
-            y_ps = tl["y", n]
+            y_ps = psum.tile([P, 2, 256], F32, tag="y", bufs=1, name="y_ps")
+            tl["y", n] = y_ps
             for gi in range(2):
                 nc.tensor.matmul_mx(
                     out=y_ps[:].rearrange("p h n -> p (h n)"),
@@ -385,17 +367,17 @@ def tile_rarevariantawarefusion_pa_t_kernel(
         wgt = const.tile([P, 32], F32, name="wgt")
         nc.gpsimd.tensor_tensor(out=wgt[:], in0=a1[:], in1=half_p[:], op=ALU.pow)
 
-        for n in range(NPAIR + 7):
+        for n in range(NPAIR + 8):
             if on(n + AHEAD):
                 load(n + AHEAD)
-            if on(n - 6):
-                turn_back(n - 6)
-            if on(n - 2):
-                leave_psum(n - 2)
+            if on(n - 7):
+                turn_back(n - 7)
             if on(n - 3):
-                bias_and_mean(n - 3)
-            if on(n - 2):
-                quantise(n - 2)
+                leave_psum(n - 3)
+            if on(n - 4):
+                bias_and_mean(n - 4)
+            if on(n - 3):
+                quantise(n - 3)
             if n == 1:
                 for gi in range(2):
                     nc.vector.quantize_mx(
@@ -403,28 +385,22 @@ def tile_rarevariantawarefusion_pa_t_kernel(
                         scales=ws[:, gi, :],
                         in_=wg[:, gi, :, :].rearrange("p n t -> p (n t)"),
                     )
-            if on(n - 1):
-                add_up(n - 1, 0)
             if on(n - 2):
-                keep_clock(n - 2)
+                add_up(n - 2)
             if on(n - 1):
-                add_up(n - 1, 1)
-            if on(n):
-                planes_scalar(n)
-            if on(n - 5):
-                gelu(n - 5)
-            if on(n - 4):
-                normalise(n - 4)
-                turn(n - 4)
-            if on(n - 2):
-                multiply(n - 2)
-            if on(n - 3):
-                variance(n - 3)
-            if on(n):
-                max_and_planes_vector(n)
-                max_plane_scalar(n)
-            if n < 4:
-                gate_step(3 + 2 * n)
-                gate_step(4 + 2 * n)
+                planes(n - 1)
             if on(n - 6):
-                residual_and_store(n - 6)
+                gelu(n - 6)
+            if on(n - 5):
+                normalise(n - 5)
+                turn(n - 5)
+            if on(n - 3):
+                multiply(n - 3)
+            if on(n - 4):
+                variance(n - 4)
+            if on(n):
+                max_and_sums(n)
+            for j in GATE_STEPS.get(n, ()):
+                gate_step(j)
+            if on(n - 7):
+                residual_and_store(n - 7)

@@ -18,9 +18,11 @@ NB = 8
 NK = 8
 D = 256
 NPAIR = 16
-NQ = 4
+NS = 3
 AHEAD = 2
-GATE_STEPS = {0: (3, 4), 1: (5, 6), 2: (7,), 3: (8,), 4: (9,)}
+GATE_STEPS = {0: (0, 1, 2), 1: (3, 4), 2: (5,), 3: (6,), 4: (7,), 5: (8,), 6: (9,)}
+L_Q = 3
+L_RES = 7
 
 
 def tile_rarevariantawarefusion_pa_t_kernel(
@@ -47,8 +49,12 @@ def tile_rarevariantawarefusion_pa_t_kernel(
             cols = slice((n % 2) * 512, (n % 2 + 1) * 512)
             r = rpool.tile([P, NK, 512], BF16, name="r")
             nc.sync.dma_start(out=r[:], in_=rv[n // 2, :, :, cols])
-            o = opool.tile([P, 512], BF16, name="o")
-            nc.sync.dma_start(out=o[:], in_=ov[n // 2, :, cols])
+            o = opool.tile([P, 2, 2, 128], BF16, name="o")
+            for c in range(2):
+                lo = (n % 2) * 512 + c * 256
+                nc.sync.dma_start(
+                    out=o[:, :, c, :], in_=ov[n // 2, :, lo : lo + 256].rearrange("p (u e) -> p u e", u=2)
+                )
             tl["r", n] = r
             tl["o", n] = o
 
@@ -68,10 +74,12 @@ def tile_rarevariantawarefusion_pa_t_kernel(
         nc.scalar.dma_start(out=vrow[2:4, :], in_=ln_g.rearrange("(r c) -> r c", r=2))
         nc.scalar.dma_start(out=vrow[4:6, :], in_=ln_b.rearrange("(r c) -> r c", r=2))
         wst = const.tile([P, 2, 4, 512], BF16, name="wst")
-        top = wf[0:256, :].rearrange("(j t) n -> j t n", t=4)
+        top = wf[0:256, :].rearrange("(u j e) n -> j u (e n)", u=2, e=2)
         bot = wf[256:512, :].rearrange("(j t) n -> j t n", t=4)
-        nc.scalar.dma_start(out=wst[0:64, 0, :, 0:256], in_=top)
-        nc.scalar.dma_start(out=wst[64:128, 0, :, 256:512], in_=top)
+        for u in range(2):
+            rows = top[:, u, :].rearrange("j (e n) -> j e n", e=2)
+            nc.scalar.dma_start(out=wst[0:64, 0, 2 * u : 2 * u + 2, 0:256], in_=rows)
+            nc.scalar.dma_start(out=wst[64:128, 0, 2 * u : 2 * u + 2, 256:512], in_=rows)
         nc.scalar.dma_start(out=wst[0:64, 1, :, 256:512], in_=bot)
         nc.scalar.dma_start(out=wst[64:128, 1, :, 0:256], in_=bot)
         bias_bc = const.tile([P, D], BF16, name="bias_bc")
@@ -87,17 +95,22 @@ def tile_rarevariantawarefusion_pa_t_kernel(
         nc.gpsimd.memset(wst[0:64, 0, :, 256:512], 0.0)
         nc.gpsimd.memset(wst[64:128, 1, :, 256:512], 0.0)
         nc.gpsimd.memset(wst[0:64, 1, :, 0:256], 0.0)
-        ones_f = const.tile([P, 2], F32, name="ones_f")
+        ones_f = const.tile([P, P], F32, name="ones_f")
         nc.vector.memset(ones_f[:], 1.0)
         half_p = const.tile([P, 32], F32, name="half_p")
         nc.vector.memset(half_p[:], 0.5)
         half_n = const.tile([P, 2], F32, name="half_n")
         nc.vector.memset(half_n[:], -0.5)
 
-        vt_ps = psum.tile([P, P], BF16, tag="f", bufs=2, name="vt_ps")
-        nc.tensor.transpose(vt_ps[:], vrow[:], ident_b[:])
         vcol = const.tile([P, 8], F32, name="vcol")
-        nc.vector.tensor_copy(out=vcol[:, 0:6], in_=vt_ps[:, 0:6])
+        b2rep = const.tile([P, 2, P], F32, name="b2rep")
+
+        def small_vectors():
+            vt_ps = psum.tile([P, P], BF16, tag="f", bufs=2, name="vt_ps")
+            nc.tensor.transpose(vt_ps[:], vrow[:], ident_b[:])
+            nc.scalar.copy(out=vcol[:, 0:6], in_=vt_ps[:, 0:6])
+            for dh in range(2):
+                nc.scalar.activation(out=b2rep[:, dh, :], in_=ones_f[:], func=ACT.Copy, scale=vcol[:, dh : dh + 1])
 
         wg = const.tile([P, 2, 512, 4], BF16, name="wg", align_bytes=64)
         wc = const.tile([P, 2, 512], U32, name="wc", align_bytes=64)
@@ -112,6 +125,7 @@ def tile_rarevariantawarefusion_pa_t_kernel(
                 op1=ALU.add,
             )
 
+        s_sb = const.tile([P, 32], F32, name="s_sb")
         sc1 = const.tile([P, 32], F32, name="sc1")
         sc2 = const.tile([P, 32], F32, name="sc2")
 
@@ -121,49 +135,50 @@ def tile_rarevariantawarefusion_pa_t_kernel(
                 for c in range(4):
                     nc.tensor.transpose(ht_ps[:, c, :], h_sb[:, j, c, :], ident_b[:])
                 ht = s1.tile([P, 512], BF16, name="ht")
-                nc.vector.tensor_copy(out=ht[:], in_=ht_ps[:].rearrange("p c i -> p (c i)"))
+                nc.scalar.copy(out=ht[:], in_=ht_ps[:].rearrange("p c i -> p (c i)"))
                 tl["ht", j] = ht
             if 0 <= j - 1 < NB:
-                sig = s1.tile([P, 2, 512], F32, name="sig")
-                for dh in range(2):
-                    z_ps = psum.tile([P, 512], F32, tag=("z1", "zt")[dh], bufs=1, name="z_ps")
-                    nc.tensor.matmul(
-                        z_ps[:],
-                        lhsT=w2_sb[:, dh * 128 : (dh + 1) * 128],
-                        rhs=tl["ht", j - 1][:],
-                        start=True,
-                        stop=True,
-                    )
-                    nc.scalar.activation(
-                        out=sig[:, dh, :], in_=z_ps[:], func=ACT.Sigmoid, bias=vcol[:, dh : dh + 1]
-                    )
-                tl["sig", j - 1] = sig
+                b = j - 1
+                for cp in range(2):
+                    z_ps = psum.tile([P, 2, D], F32, tag=("z1", "f")[cp], bufs=(1, 2)[cp], name="z_ps")
+                    for ci in range(2):
+                        c = 2 * cp + ci
+                        nc.tensor.matmul(
+                            z_ps[:, ci, :],
+                            lhsT=tl["ht", b][:, c * 128 : (c + 1) * 128],
+                            rhs=w2_sb[:],
+                            start=True,
+                            stop=False,
+                        )
+                        for dh in range(2):
+                            nc.tensor.matmul(
+                                z_ps[:, ci, dh * 128 : (dh + 1) * 128],
+                                lhsT=b2rep[:, dh, :],
+                                rhs=ident_f[:],
+                                is_transpose=True,
+                                start=False,
+                                stop=(dh == 1),
+                            )
+                    for ci in range(2):
+                        tau = b * 4 + 2 * cp + ci
+                        sjunk = s1.tile([P, D], BF16, name="sjunk")
+                        nc.scalar.activation(
+                            out=sjunk[:], in_=z_ps[:, ci, :], func=ACT.Sigmoid, accum_out=s_sb[:, tau : tau + 1]
+                        )
             if 0 <= j - 2 < NB:
                 b = j - 2
-                sig = tl["sig", b]
-                s_ps = psum.tile([P, 4], F32, tag="f", bufs=2, name="s_ps")
-                for c in range(4):
-                    for dh in range(2):
-                        nc.tensor.matmul(
-                            s_ps[:, c : c + 1],
-                            lhsT=sig[:, dh, c * 128 : (c + 1) * 128],
-                            rhs=ones_f[:, 0:1],
-                            start=(dh == 0),
-                            stop=(dh == 1),
-                        )
-                nc.vector.tensor_scalar(
-                    out=sc1[:, b * 4 : (b + 1) * 4], in0=s_ps[:], scalar1=0.7 / 8.0, scalar2=None, op0=ALU.mult
-                )
-                nc.vector.tensor_scalar(
-                    out=sc2[:, b * 4 : (b + 1) * 4], in0=s_ps[:], scalar1=0.3, scalar2=None, op0=ALU.mult
-                )
+                nc.scalar.mul(out=sc1[:, b * 4 : (b + 1) * 4], in_=s_sb[:, b * 4 : (b + 1) * 4], mul=0.7 / 8.0)
+                nc.scalar.mul(out=sc2[:, b * 4 : (b + 1) * 4], in_=s_sb[:, b * 4 : (b + 1) * 4], mul=0.3)
 
-        def max_and_sums(n):
+        def max_and_sums(n, part):
             r = tl["r", n]
-            m = work.tile([P, 4, 512], BF16, name="m", bufs=2)
-            qs = fpool.tile([P, NQ, 2, 4, 64], F32, name="qs")
-            tl["m", n] = m
-            tl["qs", n] = qs
+            if part == 0:
+                m = work.tile([P, 4, 512], BF16, name="m", bufs=2)
+                qs = fpool.tile([P, 4, 2, 4, 64], F32, name="qs")
+                tl["m", n] = m
+                tl["qs", n] = qs
+            m = tl["m", n]
+            qs = tl["qs", n]
 
             def pair_sums(cl):
                 fc = slice(cl * 256, (cl + 1) * 256)
@@ -174,14 +189,20 @@ def tile_rarevariantawarefusion_pa_t_kernel(
                     op=ALU.add,
                 )
 
-            nc.vector.tensor_tensor(out=m[:], in0=r[:, 0:4, :], in1=r[:, 4:8, :], op=ALU.max)
-            pair_sums(0)
-            nc.vector.tensor_tensor(out=m[:, 0:2, :], in0=m[:, 0:2, :], in1=m[:, 2:4, :], op=ALU.max)
-            pair_sums(1)
-            nc.vector.tensor_tensor(out=m[:, 0, :], in0=m[:, 0, :], in1=m[:, 1, :], op=ALU.max)
+            if part == 0:
+                nc.vector.tensor_tensor(out=m[:], in0=r[:, 0:4, :], in1=r[:, 4:8, :], op=ALU.max)
+                pair_sums(0)
+            if part == 1:
+                nc.vector.tensor_tensor(out=m[:, 0:2, :], in0=m[:, 0:2, :], in1=m[:, 2:4, :], op=ALU.max)
+                pair_sums(1)
+            if part == 2:
+                nc.vector.tensor_tensor(out=m[:, 0, :], in0=m[:, 0, :], in1=m[:, 1, :], op=ALU.max)
+                nc.vector.tensor_tensor(
+                    out=qs[:, 1, :, :, :], in0=qs[:, 1, :, :, :], in1=qs[:, 0, :, :, :], op=ALU.add
+                )
 
         def planes(n):
-            f = fpool.tile([P, NQ + 1, 4, 2, 64], F32, name="f")
+            f = fpool.tile([P, NS + 1, 4, 2, 64], F32, name="f")
             tl["f", n] = f
             qs = tl["qs", n]
             m = tl["m", n]
@@ -189,13 +210,13 @@ def tile_rarevariantawarefusion_pa_t_kernel(
                 cl = 1 - hb
                 tau = n * 2 + cl
                 nc.scalar.activation(
-                    out=f[:, 0:NQ, :, hb, :], in_=qs[:, :, cl, :, :], func=ACT.Copy, scale=sc1[:, tau : tau + 1]
+                    out=f[:, 0:NS, :, hb, :], in_=qs[:, 1:4, cl, :, :], func=ACT.Copy, scale=sc1[:, tau : tau + 1]
                 )
             for hb in range(2):
                 cl = 1 - hb
                 tau = n * 2 + cl
                 nc.scalar.activation(
-                    out=f[:, NQ, :, hb, :],
+                    out=f[:, NS, :, hb, :],
                     in_=m[:, 0, cl * 256 : (cl + 1) * 256].rearrange("p (j t) -> p t j", t=4),
                     func=ACT.Copy,
                     scale=sc2[:, tau : tau + 1],
@@ -206,18 +227,18 @@ def tile_rarevariantawarefusion_pa_t_kernel(
             acc_ps = psum.tile([P, 4, 128], F32, tag="acc", bufs=2, name="acc_ps")
             tl["acc", n] = acc_ps
             for t in range(4):
-                for q in range(NQ + 1):
+                for q in range(NS + 1):
                     nc.tensor.matmul(
                         acc_ps[:, t, :],
                         lhsT=f[:, q, t, :, :].rearrange("p h j -> p (h j)"),
                         rhs=ident_f[:],
                         is_transpose=True,
                         start=(q == 0),
-                        stop=(q == NQ),
+                        stop=(q == NS),
                     )
             o_ps = psum.tile([P, 2, 128], F32, tag="o", bufs=1, name="o_ps")
             tl["o_ps", n] = o_ps
-            o_words = tl["o", n][:].bitcast(F32).rearrange("p (j u) -> p u j", u=2)
+            o_words = tl["o", n][:].rearrange("p u c e -> p u (c e)").bitcast(F32)
             for u in range(2):
                 nc.tensor.transpose(o_ps[:, u, :], o_words[:, u, :], ident_f[:])
 
@@ -225,9 +246,7 @@ def tile_rarevariantawarefusion_pa_t_kernel(
             g = work.tile([P, 2, 128, 4], BF16, name="g", align_bytes=64)
             tl["g", n] = g
             nc.scalar.copy(out=g[:, 1, :, :], in_=tl["acc", n][:].rearrange("p t i -> p i t"))
-            nc.vector.tensor_copy(
-                out=g[:, 0, :, :].bitcast(F32), in_=tl["o_ps", n][:].rearrange("p u i -> p i u")
-            )
+            nc.scalar.copy(out=g[:, 0, :, :].bitcast(F32), in_=tl["o_ps", n][:].rearrange("p u i -> p i u"))
 
         def quantise(n):
             gc = work.tile([P, 256], U32, name="gc", align_bytes=64)
@@ -345,10 +364,10 @@ def tile_rarevariantawarefusion_pa_t_kernel(
             for hf in range(2):
                 tau = n * 2 + hf
                 nc.vector.scalar_tensor_tensor(
-                    out=res[:, hf, :],
-                    in0=tl["f_ps", n][:, hf, :, :].rearrange("p a d -> p (a d)"),
+                    out=res[:, hf, :].rearrange("p (a d) -> p a d", a=2),
+                    in0=tl["f_ps", n][:, hf, :, :],
                     scalar=wgt[:, tau : tau + 1],
-                    in1=tl["o", n][:, hf * 256 : (hf + 1) * 256],
+                    in1=tl["o", n][:, :, hf, :],
                     op0=ALU.mult,
                     op1=ALU.add,
                 )
@@ -358,49 +377,54 @@ def tile_rarevariantawarefusion_pa_t_kernel(
         def on(n):
             return 0 <= n < NPAIR
 
-        for j in range(3):
-            gate_step(j)
-        a1 = const.tile([P, 32], F32, name="a1")
-        a_flat = a_bf[:].rearrange("p b c -> p (b c)")
-        nc.vector.tensor_scalar(out=a1[:], in0=a_flat, scalar1=-1.0, scalar2=1.0, op0=ALU.mult, op1=ALU.add)
-        nc.vector.tensor_tensor(out=a1[:], in0=a1[:], in1=a_flat, op=ALU.mult)
-        wgt = const.tile([P, 32], F32, name="wgt")
-        nc.gpsimd.tensor_tensor(out=wgt[:], in0=a1[:], in1=half_p[:], op=ALU.pow)
+        def af_weight():
+            a_flat = a_bf[:].rearrange("p b c -> p (b c)")
+            nc.vector.tensor_scalar(out=a1[:], in0=a_flat, scalar1=-1.0, scalar2=1.0, op0=ALU.mult, op1=ALU.add)
+            nc.vector.tensor_tensor(out=a1[:], in0=a1[:], in1=a_flat, op=ALU.mult)
+            nc.gpsimd.tensor_tensor(out=wgt[:], in0=a1[:], in1=half_p[:], op=ALU.pow)
 
-        for n in range(NPAIR + 8):
+        a1 = const.tile([P, 32], F32, name="a1")
+        wgt = const.tile([P, 32], F32, name="wgt")
+
+        for n in range(NPAIR + L_RES + 1):
             if on(n + AHEAD):
                 load(n + AHEAD)
-            if on(n - 7):
-                turn_back(n - 7)
-            if on(n - 3):
-                leave_psum(n - 3)
-            if on(n - 4):
-                bias_and_mean(n - 4)
-            if on(n - 3):
-                quantise(n - 3)
-            if n == 1:
+            if on(n - L_RES):
+                turn_back(n - L_RES)
+            if on(n - L_Q):
+                leave_psum(n - L_Q)
+            if on(n - L_Q - 1):
+                bias_and_mean(n - L_Q - 1)
+            if on(n - L_Q):
+                quantise(n - L_Q)
+            if n == 2:
                 for gi in range(2):
                     nc.vector.quantize_mx(
                         out=wc[:, gi, :].bitcast(FP8X4),
                         scales=ws[:, gi, :],
                         in_=wg[:, gi, :, :].rearrange("p n t -> p (n t)"),
                     )
+                af_weight()
             if on(n - 2):
                 add_up(n - 2)
             if on(n - 1):
                 planes(n - 1)
-            if on(n - 6):
-                gelu(n - 6)
-            if on(n - 5):
-                normalise(n - 5)
-                turn(n - 5)
-            if on(n - 3):
-                multiply(n - 3)
-            if on(n - 4):
-                variance(n - 4)
-            if on(n):
-                max_and_sums(n)
-            for j in GATE_STEPS.get(n, ()):
-                gate_step(j)
-            if on(n - 7):
-                residual_and_store(n - 7)
+            if on(n - L_RES + 1):
+                gelu(n - L_RES + 1)
+            if on(n - L_RES + 2):
+                normalise(n - L_RES + 2)
+                turn(n - L_RES + 2)
+            if on(n - L_Q):
+                multiply(n - L_Q)
+            if on(n - L_RES + 3):
+                variance(n - L_RES + 3)
+            steps = GATE_STEPS.get(n, ())
+            for part in range(3):
+                if on(n):
+                    max_and_sums(n, part)
+                if n == 0 and part == 0:
+                    small_vectors()
+                if part < len(steps):
+                    gate_step(steps[part])
+            if on(n - L_RES):
+                residual_and_store(n - L_RES)

@@ -395,8 +395,12 @@ def tile_rarevariantawarefusion_pa_t_kernel(
                 leave_psum(n - L_Q)
             if on(n - L_Q - 1):
                 bias_and_mean(n - L_Q - 1)
+            if on(n):
+                max_and_sums(n, 0)
             if on(n - L_Q):
                 quantise(n - L_Q)
+            if n == 0:
+                small_vectors()
             if n == 2:
                 for gi in range(2):
                     nc.vector.quantize_mx(
@@ -405,25 +409,23 @@ def tile_rarevariantawarefusion_pa_t_kernel(
                         in_=wg[:, gi, :, :].rearrange("p n t -> p (n t)"),
                     )
                 af_weight()
-            if on(n - 2):
-                add_up(n - 2)
-            if on(n - 1):
-                planes(n - 1)
             if on(n - L_RES + 1):
                 gelu(n - L_RES + 1)
+            if on(n - 2):
+                add_up(n - 2)
+            if on(n - L_Q):
+                multiply(n - L_Q)
+            if on(n - 1):
+                planes(n - 1)
+            if on(n - L_RES + 3):
+                variance(n - L_RES + 3)
             if on(n - L_RES + 2):
                 normalise(n - L_RES + 2)
                 turn(n - L_RES + 2)
-            if on(n - L_Q):
-                multiply(n - L_Q)
-            if on(n - L_RES + 3):
-                variance(n - L_RES + 3)
             steps = GATE_STEPS.get(n, ())
             for part in range(3):
-                if on(n):
+                if on(n) and part > 0:
                     max_and_sums(n, part)
-                if n == 0 and part == 0:
-                    small_vectors()
                 if part < len(steps):
                     gate_step(steps[part])
             if on(n - L_RES):

@@ -8,6 +8,7 @@ FLOPS = 2 * 4096 * 128 * 256 + 2 * 4096 * 512 * 256
 F32 = mybir.dt.float32
 BF16 = mybir.dt.bfloat16
 U32 = mybir.dt.uint32
+I32 = mybir.dt.int32
 U8 = mybir.dt.uint8
 FP8X4 = mybir.dt.float8_e4m3fn_x4
 ALU = mybir.AluOpType
@@ -18,11 +19,14 @@ NB = 8
 NK = 8
 D = 256
 NPAIR = 16
-NS = 3
 AHEAD = 2
-GATE_STEPS = {0: (0, 1, 2), 1: (3, 4), 2: (5,), 3: (6,), 4: (7,), 5: (8,), 6: (9,)}
-L_Q = 3
-L_RES = 7
+GATE_STEPS = {0: (0, 1), 1: (2, 3), 2: (4, 5), 3: (6, 7), 4: (8,), 5: (9,), 6: (10,)}
+L_Q = 2
+L_RES = 6
+
+
+def widened(n):
+    return 2 if n < 5 else 4
 
 
 def tile_rarevariantawarefusion_pa_t_kernel(
@@ -49,21 +53,25 @@ def tile_rarevariantawarefusion_pa_t_kernel(
             cols = slice((n % 2) * 512, (n % 2 + 1) * 512)
             r = rpool.tile([P, NK, 512], BF16, name="r")
             nc.sync.dma_start(out=r[:], in_=rv[n // 2, :, :, cols])
-            o = opool.tile([P, 2, 2, 128], BF16, name="o")
-            for c in range(2):
-                lo = (n % 2) * 512 + c * 256
-                nc.sync.dma_start(
-                    out=o[:, :, c, :], in_=ov[n // 2, :, lo : lo + 256].rearrange("p (u e) -> p u e", u=2)
-                )
+            o = opool.tile([P, 512], BF16, name="o")
+            nc.sync.dma_start(out=o[:], in_=ov[n // 2, :, cols])
             tl["r", n] = r
             tl["o", n] = o
 
+        def load_h(b):
+            h = const.tile([P, 2, 4, 128], BF16, name="h%d" % b)
+            nc.sync.dma_start(
+                out=h[:].rearrange("p b c h -> p b (c h)"),
+                in_=h_af[b : b + 2].rearrange("b (i c) h -> i b (c h)", c=4),
+            )
+            for i in range(2):
+                tl["h", b + i] = h[:, i, :, :]
+
+        a_bf = const.tile([P, NB, 4], BF16, name="a_bf")
+        nc.scalar.dma_start(out=a_bf[:], in_=af.rearrange("b (i c) -> i b c", c=4))
         load(0)
-        h_sb = const.tile([P, NB, 4, 128], BF16, name="h_sb")
-        nc.sync.dma_start(
-            out=h_sb[:].rearrange("p b c h -> p b (c h)"),
-            in_=h_af.rearrange("b (i c) h -> i b (c h)", c=4),
-        )
+        load_h(0)
+        load_h(2)
         for n in range(1, AHEAD):
             load(n)
         w2_sb = const.tile([P, D], BF16, name="w2_sb")
@@ -73,34 +81,37 @@ def tile_rarevariantawarefusion_pa_t_kernel(
         nc.scalar.dma_start(out=vrow[0:2, :], in_=b2.rearrange("(r c) -> r c", r=2))
         nc.scalar.dma_start(out=vrow[2:4, :], in_=ln_g.rearrange("(r c) -> r c", r=2))
         nc.scalar.dma_start(out=vrow[4:6, :], in_=ln_b.rearrange("(r c) -> r c", r=2))
-        wst = const.tile([P, 2, 4, 512], BF16, name="wst")
-        top = wf[0:256, :].rearrange("(u j e) n -> j u (e n)", u=2, e=2)
-        bot = wf[256:512, :].rearrange("(j t) n -> j t n", t=4)
-        for u in range(2):
-            rows = top[:, u, :].rearrange("j (e n) -> j e n", e=2)
-            nc.scalar.dma_start(out=wst[0:64, 0, 2 * u : 2 * u + 2, 0:256], in_=rows)
-            nc.scalar.dma_start(out=wst[64:128, 0, 2 * u : 2 * u + 2, 256:512], in_=rows)
-        nc.scalar.dma_start(out=wst[0:64, 1, :, 256:512], in_=bot)
-        nc.scalar.dma_start(out=wst[64:128, 1, :, 0:256], in_=bot)
+        wst = const.tile([P, 2, 4, 256], BF16, name="wst")
+        for half in range(2):
+            nc.scalar.dma_start(
+                out=wst[64 * half : 64 * half + 64, :, :, :].rearrange("p g t n -> p g (t n)"),
+                in_=wf.rearrange("(g j t) n -> j g (t n)", g=2, t=4),
+            )
         bias_bc = const.tile([P, D], BF16, name="bias_bc")
         nc.scalar.dma_start(out=bias_bc[:], in_=bias_f.partition_broadcast(P))
-        a_bf = const.tile([P, NB, 4], BF16, name="a_bf")
-        nc.scalar.dma_start(out=a_bf[:], in_=af.rearrange("b (i c) -> i b c", c=4))
 
         ident_b = const.tile([P, P], BF16, name="ident_b")
         make_identity(nc, ident_b[:])
         ident_f = const.tile([P, P], F32, name="ident_f")
         make_identity(nc, ident_f[:])
-        nc.gpsimd.memset(wst[64:128, 0, :, 0:256], 0.0)
-        nc.gpsimd.memset(wst[0:64, 0, :, 256:512], 0.0)
-        nc.gpsimd.memset(wst[64:128, 1, :, 256:512], 0.0)
-        nc.gpsimd.memset(wst[0:64, 1, :, 0:256], 0.0)
         ones_f = const.tile([P, P], F32, name="ones_f")
         nc.vector.memset(ones_f[:], 1.0)
-        half_p = const.tile([P, 32], F32, name="half_p")
-        nc.vector.memset(half_p[:], 0.5)
         half_n = const.tile([P, 2], F32, name="half_n")
         nc.vector.memset(half_n[:], -0.5)
+        wcc = const.tile([P, 2, 256], U32, name="wcc", align_bytes=64)
+        wsc = const.tile([P, 2, 256], U8, name="wsc", align_bytes=64)
+        wc = const.tile([P, 2, 512], U32, name="wc", align_bytes=64)
+        ws = const.tile([P, 2, 512], U8, name="ws", align_bytes=64)
+        nc.gpsimd.memset(wsc[:].bitcast(U32), 0)
+        nc.gpsimd.memset(ws[:].bitcast(U32), 0)
+        nc.gpsimd.memset(wc[:], 0)
+
+        a_flat = a_bf[:].rearrange("p b c -> p (b c)")
+        a1 = const.tile([P, 32], F32, name="a1")
+        wgt = const.tile([P, 32], F32, name="wgt")
+        nc.vector.tensor_scalar(out=a1[:], in0=a_flat, scalar1=-1.0, scalar2=1.0, op0=ALU.mult, op1=ALU.add)
+        nc.vector.tensor_tensor(out=a1[:], in0=a1[:], in1=a_flat, op=ALU.mult)
+        nc.scalar.activation(out=wgt[:], in_=a1[:], func=ACT.Sqrt)
 
         vcol = const.tile([P, 8], F32, name="vcol")
         b2rep = const.tile([P, 2, P], F32, name="b2rep")
@@ -112,28 +123,33 @@ def tile_rarevariantawarefusion_pa_t_kernel(
             for dh in range(2):
                 nc.scalar.activation(out=b2rep[:, dh, :], in_=ones_f[:], func=ACT.Copy, scale=vcol[:, dh : dh + 1])
 
-        wg = const.tile([P, 2, 512, 4], BF16, name="wg", align_bytes=64)
-        wc = const.tile([P, 2, 512], U32, name="wc", align_bytes=64)
-        ws = const.tile([P, 2, 512], U8, name="ws", align_bytes=64)
-        for gi in range(2):
-            nc.gpsimd.tensor_scalar(
-                out=wg[:, gi, :, :],
-                in0=wst[:, gi, :, :].rearrange("p t n -> p n t"),
-                scalar1=1.0,
-                scalar2=0.0,
-                op0=ALU.mult,
-                op1=ALU.add,
+        wg = const.tile([P, 2, 256, 4], BF16, name="wg", align_bytes=64)
+
+        def weights():
+            nc.vector.quantize_mx(
+                out=wcc[:].rearrange("p g n -> p (g n)").bitcast(FP8X4),
+                scales=wsc[:].rearrange("p g n -> p (g n)"),
+                in_=wg[:].rearrange("p g n t -> p (g n t)"),
             )
 
+        def spread_weights():
+            for half in range(2):
+                rows = slice(64 * half, 64 * half + 64)
+                cols = slice(256 * half, 256 * half + 256)
+                nc.vector.tensor_copy(out=wc[rows, :, cols].bitcast(I32), in_=wcc[rows, :, :].bitcast(I32))
+                nc.vector.tensor_copy(out=ws[rows, :, cols].bitcast(I32), in_=wsc[rows, :, :].bitcast(I32))
+
         s_sb = const.tile([P, 32], F32, name="s_sb")
-        sc1 = const.tile([P, 32], F32, name="sc1")
-        sc2 = const.tile([P, 32], F32, name="sc2")
+        s_rows = const.tile([P, NPAIR, 128], F32, name="s_rows")
 
         def gate_step(j):
+            if 0 <= j - 3 < NB:
+                b = j - 3
+                nc.scalar.copy(out=s_rows[:, 2 * b : 2 * b + 2, :], in_=tl["sr", b][:])
             if j < NB:
                 ht_ps = psum.tile([P, 4, 128], BF16, tag="f", bufs=2, name="ht_ps")
                 for c in range(4):
-                    nc.tensor.transpose(ht_ps[:, c, :], h_sb[:, j, c, :], ident_b[:])
+                    nc.tensor.transpose(ht_ps[:, c, :], tl["h", j][:, c, :], ident_b[:])
                 ht = s1.tile([P, 512], BF16, name="ht")
                 nc.scalar.copy(out=ht[:], in_=ht_ps[:].rearrange("p c i -> p (c i)"))
                 tl["ht", j] = ht
@@ -167,85 +183,94 @@ def tile_rarevariantawarefusion_pa_t_kernel(
                         )
             if 0 <= j - 2 < NB:
                 b = j - 2
-                nc.scalar.mul(out=sc1[:, b * 4 : (b + 1) * 4], in_=s_sb[:, b * 4 : (b + 1) * 4], mul=0.7 / 8.0)
-                nc.scalar.mul(out=sc2[:, b * 4 : (b + 1) * 4], in_=s_sb[:, b * 4 : (b + 1) * 4], mul=0.3)
+                srep = s1.tile([P, 4, 64], F32, name="srep")
+                nc.scalar.mul(
+                    out=srep[:],
+                    in_=s_sb[:, b * 4 : (b + 1) * 4].unsqueeze(2).to_broadcast([P, 4, 64]),
+                    mul=0.7 / 8.0,
+                )
+                sr_ps = psum.tile([P, 2, 128], F32, tag="z1", bufs=1, name="sr_ps")
+                for h in range(2):
+                    nc.tensor.transpose(
+                        sr_ps[:, h, :], srep[:, 2 * h : 2 * h + 2, :].rearrange("p c j -> p (c j)"), ident_f[:]
+                    )
+                tl["sr", b] = sr_ps
+
+        def by_column(ap):
+            return ap.rearrange("p k (m t) -> p k t m", t=4)
 
         def max_and_sums(n, part):
             r = tl["r", n]
+            w = widened(n)
+            nsum = (NK - w) // 2
             if part == 0:
                 m = work.tile([P, 4, 512], BF16, name="m", bufs=2)
-                qs = fpool.tile([P, 4, 2, 4, 64], F32, name="qs")
+                f = fpool.tile([P, 7, 4, 128], F32, name="f")
                 tl["m", n] = m
-                tl["qs", n] = qs
+                tl["f", n] = f
             m = tl["m", n]
-            qs = tl["qs", n]
-
-            def pair_sums(cl):
-                fc = slice(cl * 256, (cl + 1) * 256)
-                nc.vector.tensor_tensor(
-                    out=qs[:, :, cl, :, :],
-                    in0=r[:, 0:4, fc].rearrange("p k (j t) -> p k t j", t=4),
-                    in1=r[:, 4:8, fc].rearrange("p k (j t) -> p k t j", t=4),
-                    op=ALU.add,
-                )
-
+            f = tl["f", n]
             if part == 0:
                 nc.vector.tensor_tensor(out=m[:], in0=r[:, 0:4, :], in1=r[:, 4:8, :], op=ALU.max)
-                pair_sums(0)
             if part == 1:
                 nc.vector.tensor_tensor(out=m[:, 0:2, :], in0=m[:, 0:2, :], in1=m[:, 2:4, :], op=ALU.max)
-                pair_sums(1)
+            if part == 3:
+                nc.vector.tensor_tensor(
+                    out=f[:, 0:nsum, :, :],
+                    in0=by_column(r[:, 0:nsum, :]),
+                    in1=by_column(r[:, nsum : 2 * nsum, :]),
+                    op=ALU.add,
+                )
             if part == 2:
                 nc.vector.tensor_tensor(out=m[:, 0, :], in0=m[:, 0, :], in1=m[:, 1, :], op=ALU.max)
-                nc.vector.tensor_tensor(
-                    out=qs[:, 1, :, :, :], in0=qs[:, 1, :, :, :], in1=qs[:, 0, :, :, :], op=ALU.add
+            if part == 4:
+                nc.vector.tensor_scalar(
+                    out=f[:, nsum + w, :, :],
+                    in0=m[:, 0, :].rearrange("p (m t) -> p t m", t=4),
+                    scalar1=24.0 / 7.0,
+                    scalar2=None,
+                    op0=ALU.mult,
                 )
 
-        def planes(n):
-            f = fpool.tile([P, NS + 1, 4, 2, 64], F32, name="f")
-            tl["f", n] = f
-            qs = tl["qs", n]
-            m = tl["m", n]
-            for hb in range(2):
-                cl = 1 - hb
-                tau = n * 2 + cl
-                nc.scalar.activation(
-                    out=f[:, 0:NS, :, hb, :], in_=qs[:, 1:4, cl, :, :], func=ACT.Copy, scale=sc1[:, tau : tau + 1]
-                )
-            for hb in range(2):
-                cl = 1 - hb
-                tau = n * 2 + cl
-                nc.scalar.activation(
-                    out=f[:, NS, :, hb, :],
-                    in_=m[:, 0, cl * 256 : (cl + 1) * 256].rearrange("p (j t) -> p t j", t=4),
-                    func=ACT.Copy,
-                    scale=sc2[:, tau : tau + 1],
+        def widen(n, q):
+            w = widened(n)
+            nsum = (NK - w) // 2
+            if q < w:
+                nc.scalar.copy(
+                    out=tl["f", n][:, nsum + q : nsum + q + 2, :, :],
+                    in_=by_column(tl["r", n][:, 2 * nsum + q : 2 * nsum + q + 2, :]),
                 )
 
         def add_up(n):
             f = tl["f", n]
+            planes = (NK - widened(n)) // 2 + widened(n) + 1
             acc_ps = psum.tile([P, 4, 128], F32, tag="acc", bufs=2, name="acc_ps")
             tl["acc", n] = acc_ps
             for t in range(4):
-                for q in range(NS + 1):
+                for q in range(planes):
                     nc.tensor.matmul(
                         acc_ps[:, t, :],
-                        lhsT=f[:, q, t, :, :].rearrange("p h j -> p (h j)"),
+                        lhsT=f[:, q, t, :],
                         rhs=ident_f[:],
                         is_transpose=True,
                         start=(q == 0),
-                        stop=(q == NS),
+                        stop=(q == planes - 1),
                     )
             o_ps = psum.tile([P, 2, 128], F32, tag="o", bufs=1, name="o_ps")
             tl["o_ps", n] = o_ps
-            o_words = tl["o", n][:].rearrange("p u c e -> p u (c e)").bitcast(F32)
+            o_words = tl["o", n][:].bitcast(F32)
             for u in range(2):
-                nc.tensor.transpose(o_ps[:, u, :], o_words[:, u, :], ident_f[:])
+                nc.tensor.transpose(o_ps[:, u, :], o_words[:, u:256:2], ident_f[:])
 
         def leave_psum(n):
             g = work.tile([P, 2, 128, 4], BF16, name="g", align_bytes=64)
             tl["g", n] = g
-            nc.scalar.copy(out=g[:, 1, :, :], in_=tl["acc", n][:].rearrange("p t i -> p i t"))
+            nc.vector.tensor_tensor(
+                out=g[:, 1, :, :],
+                in0=tl["acc", n][:].rearrange("p t i -> p i t"),
+                in1=s_rows[:, n, :].unsqueeze(2).to_broadcast([P, 128, 4]),
+                op=ALU.mult,
+            )
             nc.scalar.copy(out=g[:, 0, :, :].bitcast(F32), in_=tl["o_ps", n][:].rearrange("p u i -> p i u"))
 
         def quantise(n):
@@ -288,34 +313,37 @@ def tile_rarevariantawarefusion_pa_t_kernel(
                     op1=ALU.add,
                     accum_out=ysum[:, hf : hf + 1],
                 )
-            negmu = tiny.tile([P, 2], F32, name="negmu")
-            tl["negmu", n] = negmu
-            nc.vector.tensor_scalar(
-                out=negmu[:], in0=ysum[:], scalar1=-1.0 / 256.0, scalar2=None, op0=ALU.mult
-            )
+            tl["ysum", n] = ysum
 
-        def variance(n):
+        def squares(n):
             yb = tl["yb", n]
-            negmu = tl["negmu", n]
             junk = work.tile([P, 256], BF16, name="junk", bufs=2)
             ssq = tiny.tile([P, 2], F32, name="ssq")
+            tl["ssq", n] = ssq
             for hf in range(2):
                 nc.scalar.activation(
                     out=junk[:],
                     in_=yb[:, hf, :],
                     func=ACT.Square,
-                    bias=negmu[:, hf : hf + 1],
+                    scale=-256.0,
+                    bias=tl["ysum", n][:, hf : hf + 1],
                     accum_out=ssq[:, hf : hf + 1],
                 )
+
+        def inverse_deviation(n):
             ve = tiny.tile([P, 2], F32, name="ve")
-            nc.gpsimd.tensor_scalar(
-                out=ve[:], in0=ssq[:], scalar1=1.0 / 256.0, scalar2=1e-5, op0=ALU.mult, op1=ALU.add
+            nc.vector.tensor_scalar(
+                out=ve[:], in0=tl["ssq", n][:], scalar1=2.0**-24, scalar2=1e-5, op0=ALU.mult, op1=ALU.add
             )
             rstd = tiny.tile([P, 2], F32, name="rstd")
             nc.gpsimd.tensor_tensor(out=rstd[:], in0=ve[:], in1=half_n[:], op=ALU.pow)
-            nmr = tiny.tile([P, 2], F32, name="nmr")
-            nc.gpsimd.tensor_tensor(out=nmr[:], in0=negmu[:], in1=rstd[:], op=ALU.mult)
             tl["rstd", n] = rstd
+
+        def shift(n):
+            nmr = tiny.tile([P, 2], F32, name="nmr")
+            nc.vector.scalar_tensor_tensor(
+                out=nmr[:], in0=tl["ysum", n][:], scalar=-1.0 / 256.0, in1=tl["rstd", n][:], op0=ALU.mult, op1=ALU.mult
+            )
             tl["nmr", n] = nmr
 
         def normalise(n):
@@ -364,10 +392,10 @@ def tile_rarevariantawarefusion_pa_t_kernel(
             for hf in range(2):
                 tau = n * 2 + hf
                 nc.vector.scalar_tensor_tensor(
-                    out=res[:, hf, :].rearrange("p (a d) -> p a d", a=2),
-                    in0=tl["f_ps", n][:, hf, :, :],
+                    out=res[:, hf, :],
+                    in0=tl["f_ps", n][:, hf, :, :].rearrange("p a d -> p (a d)"),
                     scalar=wgt[:, tau : tau + 1],
-                    in1=tl["o", n][:, :, hf, :],
+                    in1=tl["o", n][:, hf * 256 : (hf + 1) * 256],
                     op0=ALU.mult,
                     op1=ALU.add,
                 )
@@ -377,56 +405,56 @@ def tile_rarevariantawarefusion_pa_t_kernel(
         def on(n):
             return 0 <= n < NPAIR
 
-        def af_weight():
-            a_flat = a_bf[:].rearrange("p b c -> p (b c)")
-            nc.vector.tensor_scalar(out=a1[:], in0=a_flat, scalar1=-1.0, scalar2=1.0, op0=ALU.mult, op1=ALU.add)
-            nc.vector.tensor_tensor(out=a1[:], in0=a1[:], in1=a_flat, op=ALU.mult)
-            nc.gpsimd.tensor_tensor(out=wgt[:], in0=a1[:], in1=half_p[:], op=ALU.pow)
-
-        a1 = const.tile([P, 32], F32, name="a1")
-        wgt = const.tile([P, 32], F32, name="wgt")
-
         for n in range(NPAIR + L_RES + 1):
             if on(n + AHEAD):
                 load(n + AHEAD)
+            if n in (0, 1):
+                load_h(4 + 2 * n)
+            if n == 0:
+                small_vectors()
+            if on(n):
+                max_and_sums(n, 0)
+            if on(n - L_Q - 2):
+                inverse_deviation(n - L_Q - 2)
             if on(n - L_RES):
                 turn_back(n - L_RES)
             if on(n - L_Q):
                 leave_psum(n - L_Q)
             if on(n - L_Q - 1):
                 bias_and_mean(n - L_Q - 1)
+            if on(n - L_RES):
+                residual_and_store(n - L_RES)
+            if on(n - L_Q - 2):
+                shift(n - L_Q - 2)
             if on(n):
-                max_and_sums(n, 0)
+                max_and_sums(n, 1)
             if on(n - L_Q):
                 quantise(n - L_Q)
-            if n == 0:
-                small_vectors()
-            if n == 2:
-                for gi in range(2):
-                    nc.vector.quantize_mx(
-                        out=wc[:, gi, :].bitcast(FP8X4),
-                        scales=ws[:, gi, :],
-                        in_=wg[:, gi, :, :].rearrange("p n t -> p (n t)"),
-                    )
-                af_weight()
+            if on(n):
+                max_and_sums(n, 2)
+            if n == 1:
+                weights()
+            if on(n):
+                max_and_sums(n, 3)
+                max_and_sums(n, 4)
+            if n == 1:
+                spread_weights()
             if on(n - L_RES + 1):
                 gelu(n - L_RES + 1)
-            if on(n - 2):
-                add_up(n - 2)
+            if on(n - 1):
+                add_up(n - 1)
             if on(n - L_Q):
                 multiply(n - L_Q)
-            if on(n - 1):
-                planes(n - 1)
-            if on(n - L_RES + 3):
-                variance(n - L_RES + 3)
+            if on(n):
+                widen(n, 0)
+            if on(n - L_Q - 1):
+                squares(n - L_Q - 1)
+            if on(n):
+                widen(n, 2)
             if on(n - L_RES + 2):
                 normalise(n - L_RES + 2)
                 turn(n - L_RES + 2)
-            steps = GATE_STEPS.get(n, ())
-            for part in range(3):
-                if on(n) and part > 0:
-                    max_and_sums(n, part)
-                if part < len(steps):
-                    gate_step(steps[part])
-            if on(n - L_RES):
-                residual_and_store(n - L_RES)
+            for j in GATE_STEPS.get(n, ()):
+                gate_step(j)
+            if n == 0:
+                nc.scalar.copy(out=wg[:], in_=wst[:].rearrange("p g t n -> p g n t"))

@@ -20,13 +20,13 @@ NK = 8
 D = 256
 NPAIR = 16
 AHEAD = 2
-GATE_STEPS = {0: (0, 1), 1: (2, 3), 2: (4, 5), 3: (6, 7), 4: (8,), 5: (9,), 6: (10,)}
+GATE_STEPS = {0: (0, 1), 1: (2, 3), 2: (4, 5), 3: (6, 7), 4: (8, 9)}
 L_Q = 2
 L_RES = 6
 
 
 def widened(n):
-    return 2 if n < 5 else 4
+    return 0 if n < 4 else 2 if n == 4 else 4
 
 
 def tile_rarevariantawarefusion_pa_t_kernel(
@@ -83,12 +83,12 @@ def tile_rarevariantawarefusion_pa_t_kernel(
         nc.scalar.dma_start(out=vrow[4:6, :], in_=ln_b.rearrange("(r c) -> r c", r=2))
         wst = const.tile([P, 2, 4, 256], BF16, name="wst")
         for half in range(2):
-            nc.scalar.dma_start(
+            nc.gpsimd.dma_start(
                 out=wst[64 * half : 64 * half + 64, :, :, :].rearrange("p g t n -> p g (t n)"),
                 in_=wf.rearrange("(g j t) n -> j g (t n)", g=2, t=4),
             )
         bias_bc = const.tile([P, D], BF16, name="bias_bc")
-        nc.scalar.dma_start(out=bias_bc[:], in_=bias_f.partition_broadcast(P))
+        nc.gpsimd.dma_start(out=bias_bc[:], in_=bias_f.partition_broadcast(P))
 
         ident_b = const.tile([P, P], BF16, name="ident_b")
         make_identity(nc, ident_b[:])
@@ -142,21 +142,17 @@ def tile_rarevariantawarefusion_pa_t_kernel(
         s_sb = const.tile([P, 32], F32, name="s_sb")
         s_rows = const.tile([P, NPAIR, 128], F32, name="s_rows")
 
-        def gate_step(j):
-            if 0 <= j - 3 < NB:
-                b = j - 3
-                nc.scalar.copy(out=s_rows[:, 2 * b : 2 * b + 2, :], in_=tl["sr", b][:])
+        def gate_tensor(j):
             if j < NB:
                 ht_ps = psum.tile([P, 4, 128], BF16, tag="f", bufs=2, name="ht_ps")
                 for c in range(4):
                     nc.tensor.transpose(ht_ps[:, c, :], tl["h", j][:, c, :], ident_b[:])
-                ht = s1.tile([P, 512], BF16, name="ht")
-                nc.scalar.copy(out=ht[:], in_=ht_ps[:].rearrange("p c i -> p (c i)"))
-                tl["ht", j] = ht
+                tl["ht_ps", j] = ht_ps
             if 0 <= j - 1 < NB:
                 b = j - 1
                 for cp in range(2):
                     z_ps = psum.tile([P, 2, D], F32, tag=("z1", "f")[cp], bufs=(1, 2)[cp], name="z_ps")
+                    tl["z_ps", b, cp] = z_ps
                     for ci in range(2):
                         c = 2 * cp + ci
                         nc.tensor.matmul(
@@ -175,26 +171,44 @@ def tile_rarevariantawarefusion_pa_t_kernel(
                                 start=False,
                                 stop=(dh == 1),
                             )
-                    for ci in range(2):
-                        tau = b * 4 + 2 * cp + ci
-                        sjunk = s1.tile([P, D], BF16, name="sjunk")
-                        nc.scalar.activation(
-                            out=sjunk[:], in_=z_ps[:, ci, :], func=ACT.Sigmoid, accum_out=s_sb[:, tau : tau + 1]
-                        )
             if 0 <= j - 2 < NB:
                 b = j - 2
+                sr_ps = psum.tile([P, 2, 128], F32, tag="zt", bufs=1, name="sr_ps")
+                tl["sr_ps", b] = sr_ps
+                for h in range(2):
+                    nc.tensor.transpose(
+                        sr_ps[:, h, :],
+                        tl["srep", b][:, 2 * h : 2 * h + 2, :].rearrange("p c j -> p (c j)"),
+                        ident_f[:],
+                    )
+
+        def gate_scalar(j):
+            if j < NB:
+                ht = s1.tile([P, 512], BF16, name="ht")
+                nc.scalar.copy(out=ht[:], in_=tl["ht_ps", j][:].rearrange("p c i -> p (c i)"))
+                tl["ht", j] = ht
+            if 0 <= j - 1 < NB:
+                b = j - 1
+                for c in range(4):
+                    sjunk = s1.tile([P, D], BF16, name="sjunk")
+                    nc.scalar.activation(
+                        out=sjunk[:],
+                        in_=tl["z_ps", b, c // 2][:, c % 2, :],
+                        func=ACT.Sigmoid,
+                        accum_out=s_sb[:, b * 4 + c : b * 4 + c + 1],
+                    )
+            if 0 <= j - 2 < NB:
+                b = j - 2
+                nc.scalar.copy(out=s_rows[:, 2 * b : 2 * b + 2, :], in_=tl["sr_ps", b][:])
+            if 0 <= j - 1 < NB:
+                b = j - 1
                 srep = s1.tile([P, 4, 64], F32, name="srep")
+                tl["srep", b] = srep
                 nc.scalar.mul(
                     out=srep[:],
                     in_=s_sb[:, b * 4 : (b + 1) * 4].unsqueeze(2).to_broadcast([P, 4, 64]),
                     mul=0.7 / 8.0,
                 )
-                sr_ps = psum.tile([P, 2, 128], F32, tag="z1", bufs=1, name="sr_ps")
-                for h in range(2):
-                    nc.tensor.transpose(
-                        sr_ps[:, h, :], srep[:, 2 * h : 2 * h + 2, :].rearrange("p c j -> p (c j)"), ident_f[:]
-                    )
-                tl["sr", b] = sr_ps
 
         def by_column(ap):
             return ap.rearrange("p k (m t) -> p k t m", t=4)
@@ -241,12 +255,14 @@ def tile_rarevariantawarefusion_pa_t_kernel(
                     in_=by_column(tl["r", n][:, 2 * nsum + q : 2 * nsum + q + 2, :]),
                 )
 
-        def add_up(n):
+        def add_up(n, ts):
             f = tl["f", n]
             planes = (NK - widened(n)) // 2 + widened(n) + 1
-            acc_ps = psum.tile([P, 4, 128], F32, tag="acc", bufs=2, name="acc_ps")
-            tl["acc", n] = acc_ps
-            for t in range(4):
+            if 0 in ts:
+                acc_ps = psum.tile([P, 4, 128], F32, tag="acc", bufs=2, name="acc_ps")
+                tl["acc", n] = acc_ps
+            acc_ps = tl["acc", n]
+            for t in ts:
                 for q in range(planes):
                     nc.tensor.matmul(
                         acc_ps[:, t, :],
@@ -256,6 +272,8 @@ def tile_rarevariantawarefusion_pa_t_kernel(
                         start=(q == 0),
                         stop=(q == planes - 1),
                     )
+
+        def turn_orig(n):
             o_ps = psum.tile([P, 2, 128], F32, tag="o", bufs=1, name="o_ps")
             tl["o_ps", n] = o_ps
             o_words = tl["o", n][:].bitcast(F32)
@@ -406,6 +424,7 @@ def tile_rarevariantawarefusion_pa_t_kernel(
             return 0 <= n < NPAIR
 
         for n in range(NPAIR + L_RES + 1):
+            steps = GATE_STEPS.get(n)
             if on(n + AHEAD):
                 load(n + AHEAD)
             if n in (0, 1):
@@ -418,6 +437,8 @@ def tile_rarevariantawarefusion_pa_t_kernel(
                 inverse_deviation(n - L_Q - 2)
             if on(n - L_RES):
                 turn_back(n - L_RES)
+            if steps:
+                gate_tensor(steps[0])
             if on(n - L_Q):
                 leave_psum(n - L_Q)
             if on(n - L_Q - 1):
@@ -441,20 +462,27 @@ def tile_rarevariantawarefusion_pa_t_kernel(
                 spread_weights()
             if on(n - L_RES + 1):
                 gelu(n - L_RES + 1)
+            if steps:
+                gate_scalar(steps[0])
             if on(n - 1):
-                add_up(n - 1)
+                add_up(n - 1, (0, 1))
+            if steps:
+                gate_tensor(steps[1])
+            if on(n - 1):
+                add_up(n - 1, (2, 3))
+                turn_orig(n - 1)
             if on(n - L_Q):
                 multiply(n - L_Q)
             if on(n):
                 widen(n, 0)
             if on(n - L_Q - 1):
                 squares(n - L_Q - 1)
+            if steps:
+                gate_scalar(steps[1])
             if on(n):
                 widen(n, 2)
             if on(n - L_RES + 2):
                 normalise(n - L_RES + 2)
                 turn(n - L_RES + 2)
-            for j in GATE_STEPS.get(n, ()):
-                gate_step(j)
             if n == 0:
                 nc.scalar.copy(out=wg[:], in_=wst[:].rearrange("p g t n -> p g n t"))

@@ -261,6 +261,8 @@ def tile_rarevariantawarefusion_pa_t_kernel(
             if 0 in ts:
                 acc_ps = psum.tile([P, 4, 128], F32, tag="acc", bufs=2, name="acc_ps")
                 tl["acc", n] = acc_ps
+                if n > 0:
+                    keep_warm(acc_ps[:].rearrange("p t i -> p (t i)"))
             acc_ps = tl["acc", n]
             for t in ts:
                 for q in range(planes):
@@ -300,11 +302,15 @@ def tile_rarevariantawarefusion_pa_t_kernel(
                 out=gc[:].bitcast(FP8X4), scales=gs[:], in_=tl["g", n][:].rearrange("p g i t -> p (g i t)")
             )
 
+        def open_product(n):
+            y_ps = psum.tile([P, 2, 256], F32, tag="y", bufs=1, name="y_ps")
+            tl["y", n] = y_ps
+            keep_warm(y_ps[:].rearrange("p h n -> p (h n)"))
+
         def multiply(n):
             gc = tl["gc", n]
             gs = tl["gs", n]
-            y_ps = psum.tile([P, 2, 256], F32, tag="y", bufs=1, name="y_ps")
-            tl["y", n] = y_ps
+            y_ps = tl["y", n]
             for gi in range(2):
                 nc.tensor.matmul_mx(
                     out=y_ps[:].rearrange("p h n -> p (h n)"),
@@ -314,6 +320,18 @@ def tile_rarevariantawarefusion_pa_t_kernel(
                     rhs_scale=ws[:, gi, :],
                     start=(gi == 0),
                     stop=(gi == 1),
+                )
+
+        def keep_warm(bank):
+            for i in range(2):
+                nc.tensor.matmul_mx(
+                    out=bank,
+                    lhsT=wc[:, i, 0:128].bitcast(FP8X4),
+                    lhsT_scale=ws[:, i, 0:128],
+                    rhs=wc[:, i, :].bitcast(FP8X4),
+                    rhs_scale=ws[:, i, :],
+                    start=True,
+                    stop=True,
                 )
 
         def bias_and_mean(n):
@@ -405,20 +423,23 @@ def tile_rarevariantawarefusion_pa_t_kernel(
                 for dh in range(2):
                     nc.tensor.transpose(f_ps[:, hf, dh, :], get[:, dh, hf, :], ident_f[:])
 
-        def residual_and_store(n):
-            res = work.tile([P, 2, 256], F32, name="res")
-            for hf in range(2):
-                tau = n * 2 + hf
-                nc.vector.scalar_tensor_tensor(
-                    out=res[:, hf, :],
-                    in0=tl["f_ps", n][:, hf, :, :].rearrange("p a d -> p (a d)"),
-                    scalar=wgt[:, tau : tau + 1],
-                    in1=tl["o", n][:, hf * 256 : (hf + 1) * 256],
-                    op0=ALU.mult,
-                    op1=ALU.add,
-                )
-            cols = slice((n % 2) * 512, (n % 2 + 1) * 512)
-            nc.sync.dma_start(out=outv[n // 2, :, cols], in_=res[:].rearrange("p h d -> p (h d)"))
+        def residual_and_store(n, hf):
+            if hf == 0:
+                res = work.tile([P, 2, 256], F32, name="res")
+                tl["res", n] = res
+            res = tl["res", n]
+            tau = n * 2 + hf
+            nc.vector.scalar_tensor_tensor(
+                out=res[:, hf, :],
+                in0=tl["f_ps", n][:, hf, :, :].rearrange("p a d -> p (a d)"),
+                scalar=wgt[:, tau : tau + 1],
+                in1=tl["o", n][:, hf * 256 : (hf + 1) * 256],
+                op0=ALU.mult,
+                op1=ALU.add,
+            )
+            if hf == 1:
+                cols = slice((n % 2) * 512, (n % 2 + 1) * 512)
+                nc.sync.dma_start(out=outv[n // 2, :, cols], in_=res[:].rearrange("p h d -> p (h d)"))
 
         def on(n):
             return 0 <= n < NPAIR
@@ -443,14 +464,16 @@ def tile_rarevariantawarefusion_pa_t_kernel(
                 leave_psum(n - L_Q)
             if on(n - L_Q - 1):
                 bias_and_mean(n - L_Q - 1)
-            if on(n - L_RES):
-                residual_and_store(n - L_RES)
-            if on(n - L_Q - 2):
-                shift(n - L_Q - 2)
-            if on(n):
-                max_and_sums(n, 1)
             if on(n - L_Q):
                 quantise(n - L_Q)
+            if on(n - L_Q - 2):
+                shift(n - L_Q - 2)
+            if on(n - L_RES):
+                residual_and_store(n - L_RES, 0)
+            if on(n):
+                max_and_sums(n, 1)
+            if on(n - L_RES):
+                residual_and_store(n - L_RES, 1)
             if on(n):
                 max_and_sums(n, 2)
             if n == 1:
@@ -468,6 +491,8 @@ def tile_rarevariantawarefusion_pa_t_kernel(
                 add_up(n - 1, (0, 1))
             if steps:
                 gate_tensor(steps[1])
+            if on(n - L_Q):
+                open_product(n - L_Q)
             if on(n - 1):
                 add_up(n - 1, (2, 3))
                 turn_orig(n - 1)

@@ -20,13 +20,20 @@ NK = 8
 D = 256
 NPAIR = 16
 AHEAD = 2
-GATE_STEPS = {0: (0, 1), 1: (2, 3), 2: (4, 5), 3: (6, 7), 4: (8, 9)}
+GATE_STEPS = {0: (0, 1), **{n: (n + 1,) for n in range(1, NB + 1)}}
 L_Q = 2
+L_NORM = 4
+L_GELU = 5
 L_RES = 6
+GELU_FROM = NB
 
 
 def widened(n):
-    return 0 if n < 4 else 2 if n == 4 else 4
+    return 0 if n == 0 else 2 if n < GELU_FROM else 4
+
+
+def gelu_slot(n):
+    return max(n + L_GELU, GELU_FROM + n // 2)
 
 
 def tile_rarevariantawarefusion_pa_t_kernel(
@@ -37,7 +44,7 @@ def tile_rarevariantawarefusion_pa_t_kernel(
         const = ctx.enter_context(tc.tile_pool(name="const", bufs=1))
         s1 = ctx.enter_context(tc.tile_pool(name="s1", bufs=2))
         rpool = ctx.enter_context(tc.tile_pool(name="rpool", bufs=4))
-        opool = ctx.enter_context(tc.tile_pool(name="opool", bufs=11))
+        opool = ctx.enter_context(tc.tile_pool(name="opool", bufs=13))
         fpool = ctx.enter_context(tc.tile_pool(name="fpool", bufs=3))
         work = ctx.enter_context(tc.tile_pool(name="work", bufs=3))
         tiny = ctx.enter_context(tc.tile_pool(name="tiny", bufs=4))
@@ -52,7 +59,9 @@ def tile_rarevariantawarefusion_pa_t_kernel(
         def load(n):
             cols = slice((n % 2) * 512, (n % 2 + 1) * 512)
             r = rpool.tile([P, NK, 512], BF16, name="r")
-            nc.sync.dma_start(out=r[:], in_=rv[n // 2, :, :, cols])
+            for ks in ((0, 4, 2, 6) if n == 0 else (0,)):
+                k1 = ks + (2 if n == 0 else NK)
+                nc.sync.dma_start(out=r[:, ks:k1, :], in_=rv[n // 2, :, ks:k1, cols])
             o = opool.tile([P, 512], BF16, name="o")
             nc.sync.dma_start(out=o[:], in_=ov[n // 2, :, cols])
             tl["r", n] = r
@@ -109,9 +118,15 @@ def tile_rarevariantawarefusion_pa_t_kernel(
         a_flat = a_bf[:].rearrange("p b c -> p (b c)")
         a1 = const.tile([P, 32], F32, name="a1")
         wgt = const.tile([P, 32], F32, name="wgt")
-        nc.vector.tensor_scalar(out=a1[:], in0=a_flat, scalar1=-1.0, scalar2=1.0, op0=ALU.mult, op1=ALU.add)
-        nc.vector.tensor_tensor(out=a1[:], in0=a1[:], in1=a_flat, op=ALU.mult)
-        nc.scalar.activation(out=wgt[:], in_=a1[:], func=ACT.Sqrt)
+
+        def af_product():
+            nc.vector.tensor_scalar(out=a1[:], in0=a_flat, scalar1=-1.0, scalar2=1.0, op0=ALU.mult, op1=ALU.add)
+            nc.vector.tensor_tensor(out=a1[:], in0=a1[:], in1=a_flat, op=ALU.mult)
+
+        def af_weight():
+            nc.scalar.activation(out=wgt[:], in_=a1[:], func=ACT.Sqrt)
+
+        nc.scalar.activation(out=wgt[:, 0:1], in_=ones_f[:, 0:1], func=ACT.Sqrt)
 
         vcol = const.tile([P, 8], F32, name="vcol")
         b2rep = const.tile([P, 2, P], F32, name="b2rep")
@@ -225,7 +240,11 @@ def tile_rarevariantawarefusion_pa_t_kernel(
             m = tl["m", n]
             f = tl["f", n]
             if part == 0:
-                nc.vector.tensor_tensor(out=m[:], in0=r[:, 0:4, :], in1=r[:, 4:8, :], op=ALU.max)
+                step = 2 if n == 0 else 4
+                for k in range(0, 4, step):
+                    nc.vector.tensor_tensor(
+                        out=m[:, k : k + step, :], in0=r[:, k : k + step, :], in1=r[:, k + 4 : k + 4 + step, :], op=ALU.max
+                    )
             if part == 1:
                 nc.vector.tensor_tensor(out=m[:, 0:2, :], in0=m[:, 0:2, :], in1=m[:, 2:4, :], op=ALU.max)
             if part == 3:
@@ -261,8 +280,6 @@ def tile_rarevariantawarefusion_pa_t_kernel(
             if 0 in ts:
                 acc_ps = psum.tile([P, 4, 128], F32, tag="acc", bufs=2, name="acc_ps")
                 tl["acc", n] = acc_ps
-                if n > 0:
-                    keep_warm(acc_ps[:].rearrange("p t i -> p (t i)"))
             acc_ps = tl["acc", n]
             for t in ts:
                 for q in range(planes):
@@ -305,7 +322,8 @@ def tile_rarevariantawarefusion_pa_t_kernel(
         def open_product(n):
             y_ps = psum.tile([P, 2, 256], F32, tag="y", bufs=1, name="y_ps")
             tl["y", n] = y_ps
-            keep_warm(y_ps[:].rearrange("p h n -> p (h n)"))
+            if n < NPAIR - 1:
+                keep_warm(y_ps[:].rearrange("p h n -> p (h n)"))
 
         def multiply(n):
             gc = tl["gc", n]
@@ -384,7 +402,7 @@ def tile_rarevariantawarefusion_pa_t_kernel(
 
         def normalise(n):
             yb = tl["yb", n]
-            z = work.tile([P, 2, 256], F32, name="z", bufs=2)
+            z = work.tile([P, 2, 256], F32, name="z", bufs=5)
             tl["z", n] = z
             for hf in range(2):
                 nc.scalar.activation(
@@ -395,16 +413,16 @@ def tile_rarevariantawarefusion_pa_t_kernel(
                     bias=tl["nmr", n][:, hf : hf + 1],
                 )
 
-        def turn(n):
+        def turn(n, tag):
             z = tl["z", n]
-            zt_ps = psum.tile([P, 2, 2, 128], F32, tag="zt", bufs=1, name="zt_ps")
+            zt_ps = psum.tile([P, 2, 2, 128], F32, tag=tag, bufs=1, name="zt_ps")
             tl["zt", n] = zt_ps
             for dh in range(2):
                 for hf in range(2):
                     nc.tensor.transpose(zt_ps[:, dh, hf, :], z[:, hf, dh * 128 : (dh + 1) * 128], ident_f[:])
 
         def gelu(n):
-            get = work.tile([P, 2, 2, 128], F32, name="get", bufs=2)
+            get = work.tile([P, 2, 2, 128], F32, name="get", bufs=4)
             tl["get", n] = get
             for dh in range(2):
                 nc.scalar.activation(
@@ -445,7 +463,10 @@ def tile_rarevariantawarefusion_pa_t_kernel(
             return 0 <= n < NPAIR
 
         for n in range(NPAIR + L_RES + 1):
-            steps = GATE_STEPS.get(n)
+            steps = GATE_STEPS.get(n, ())
+            back = [p for p in range(NPAIR) if gelu_slot(p) == n - 1]
+            gelus = [p for p in range(NPAIR) if gelu_slot(p) == n]
+            turns = [p for p in range(NPAIR) if gelu_slot(p) == n + 1]
             if on(n + AHEAD):
                 load(n + AHEAD)
             if n in (0, 1):
@@ -454,60 +475,70 @@ def tile_rarevariantawarefusion_pa_t_kernel(
                 small_vectors()
             if on(n):
                 max_and_sums(n, 0)
-            if on(n - L_Q - 2):
-                inverse_deviation(n - L_Q - 2)
-            if on(n - L_RES):
-                turn_back(n - L_RES)
+            if on(n - L_NORM):
+                inverse_deviation(n - L_NORM)
+            for p in back:
+                turn_back(p)
             if steps:
                 gate_tensor(steps[0])
+            last = n == NPAIR - 1
             if on(n - L_Q):
                 leave_psum(n - L_Q)
-            if on(n - L_Q - 1):
+            if n == 2:
+                spread_weights()
+            if on(n - L_Q - 1) and not last:
                 bias_and_mean(n - L_Q - 1)
+            if last:
+                max_and_sums(n, 1)
             if on(n - L_Q):
                 quantise(n - L_Q)
-            if on(n - L_Q - 2):
-                shift(n - L_Q - 2)
-            if on(n - L_RES):
-                residual_and_store(n - L_RES, 0)
-            if on(n):
-                max_and_sums(n, 1)
-            if on(n - L_RES):
-                residual_and_store(n - L_RES, 1)
+            if on(n - L_NORM):
+                shift(n - L_NORM)
+            if not last:
+                for p in back:
+                    residual_and_store(p, 0)
+                if on(n):
+                    max_and_sums(n, 1)
+                for p in back:
+                    residual_and_store(p, 1)
+            if n == 0:
+                af_product()
             if on(n):
                 max_and_sums(n, 2)
-            if n == 1:
-                weights()
-            if on(n):
                 max_and_sums(n, 3)
                 max_and_sums(n, 4)
+            if last:
+                bias_and_mean(n - L_Q - 1)
+                for p in back:
+                    residual_and_store(p, 0)
+                    residual_and_store(p, 1)
             if n == 1:
-                spread_weights()
-            if on(n - L_RES + 1):
-                gelu(n - L_RES + 1)
+                weights()
+            for p in gelus:
+                gelu(p)
             if steps:
                 gate_scalar(steps[0])
+            if n == 0:
+                af_weight()
+            for j in steps[1:]:
+                gate_tensor(j)
             if on(n - 1):
-                add_up(n - 1, (0, 1))
-            if steps:
-                gate_tensor(steps[1])
-            if on(n - L_Q):
-                open_product(n - L_Q)
-            if on(n - 1):
-                add_up(n - 1, (2, 3))
+                add_up(n - 1, (0, 1, 2, 3))
                 turn_orig(n - 1)
             if on(n - L_Q):
+                open_product(n - L_Q)
                 multiply(n - L_Q)
             if on(n):
                 widen(n, 0)
             if on(n - L_Q - 1):
                 squares(n - L_Q - 1)
-            if steps:
-                gate_scalar(steps[1])
+            for j in steps[1:]:
+                gate_scalar(j)
             if on(n):
                 widen(n, 2)
-            if on(n - L_RES + 2):
-                normalise(n - L_RES + 2)
-                turn(n - L_RES + 2)
+            if on(n - L_NORM):
+                normalise(n - L_NORM)
+            for p, tag in zip(turns, ("zt", "z1")):
+                turn(p, tag)
             if n == 0:
                 nc.scalar.copy(out=wg[:], in_=wst[:].rearrange("p g t n -> p g n t"))

@@ -392,13 +392,16 @@ def tile_rarevariantawarefusion_pa_t_kernel(
             rstd = tiny.tile([P, 2], F32, name="rstd")
             nc.gpsimd.tensor_tensor(out=rstd[:], in0=ve[:], in1=half_n[:], op=ALU.pow)
             tl["rstd", n] = rstd
-
-        def shift(n):
             nmr = tiny.tile([P, 2], F32, name="nmr")
-            nc.vector.scalar_tensor_tensor(
-                out=nmr[:], in0=tl["ysum", n][:], scalar=-1.0 / 256.0, in1=tl["rstd", n][:], op0=ALU.mult, op1=ALU.mult
-            )
+            nc.gpsimd.tensor_tensor(out=nmr[:], in0=tl["negmu", n][:], in1=rstd[:], op=ALU.mult)
             tl["nmr", n] = nmr
+
+        def negative_mean(n):
+            negmu = tiny.tile([P, 2], F32, name="negmu")
+            nc.vector.tensor_scalar(
+                out=negmu[:], in0=tl["ysum", n][:], scalar1=-1.0 / 256.0, scalar2=None, op0=ALU.mult
+            )
+            tl["negmu", n] = negmu
 
         def normalise(n):
             yb = tl["yb", n]
@@ -486,31 +489,31 @@ def tile_rarevariantawarefusion_pa_t_kernel(
                 leave_psum(n - L_Q)
             if n == 2:
                 spread_weights()
-            if on(n - L_Q - 1) and not last:
+            if on(n - L_Q - 1):
                 bias_and_mean(n - L_Q - 1)
-            if last:
-                max_and_sums(n, 1)
             if on(n - L_Q):
                 quantise(n - L_Q)
-            if on(n - L_NORM):
-                shift(n - L_NORM)
+            if on(n - L_Q - 1):
+                negative_mean(n - L_Q - 1)
             if not last:
                 for p in back:
                     residual_and_store(p, 0)
-                if on(n):
-                    max_and_sums(n, 1)
+            if on(n):
+                max_and_sums(n, 1)
+            if not last:
                 for p in back:
                     residual_and_store(p, 1)
             if n == 0:
                 af_product()
             if on(n):
-                max_and_sums(n, 2)
                 max_and_sums(n, 3)
+                max_and_sums(n, 2)
+                if last:
+                    for p in back:
+                        residual_and_store(p, 0)
                 max_and_sums(n, 4)
             if last:
-                bias_and_mean(n - L_Q - 1)
                 for p in back:
-                    residual_and_store(p, 0)
                     residual_and_store(p, 1)
             if n == 1:
                 weights()

@@ -22,14 +22,16 @@ NPAIR = 16
 AHEAD = 2
 GATE_STEPS = {0: (0, 1), **{n: (n + 1,) for n in range(1, NB + 1)}}
 L_Q = 2
-L_NORM = 4
-L_GELU = 5
-L_RES = 6
+L_Y = 3
+L_SQ = 4
+L_NORM = 5
+L_GELU = 6
+L_END = 12
 GELU_FROM = NB
 
 
 def widened(n):
-    return 0 if n == 0 else 2 if n < GELU_FROM else 4
+    return 0 if n == 0 else 2 if n < GELU_FROM + 2 else 4
 
 
 def gelu_slot(n):
@@ -44,10 +46,10 @@ def tile_rarevariantawarefusion_pa_t_kernel(
         const = ctx.enter_context(tc.tile_pool(name="const", bufs=1))
         s1 = ctx.enter_context(tc.tile_pool(name="s1", bufs=2))
         rpool = ctx.enter_context(tc.tile_pool(name="rpool", bufs=4))
-        opool = ctx.enter_context(tc.tile_pool(name="opool", bufs=13))
+        opool = ctx.enter_context(tc.tile_pool(name="opool", bufs=16))
         fpool = ctx.enter_context(tc.tile_pool(name="fpool", bufs=3))
         work = ctx.enter_context(tc.tile_pool(name="work", bufs=3))
-        tiny = ctx.enter_context(tc.tile_pool(name="tiny", bufs=4))
+        tiny = ctx.enter_context(tc.tile_pool(name="tiny", bufs=6))
         psum = ctx.enter_context(tc.psum_pool(name="psum", bufs=1))
         ctx.enter_context(tc.manual_schedule())
 
@@ -188,7 +190,7 @@ def tile_rarevariantawarefusion_pa_t_kernel(
                             )
             if 0 <= j - 2 < NB:
                 b = j - 2
-                sr_ps = psum.tile([P, 2, 128], F32, tag="zt", bufs=1, name="sr_ps")
+                sr_ps = psum.tile([P, 2, 128], F32, tag="zt" if j <= NB else "f", bufs=1 if j <= NB else 2, name="sr_ps")
                 tl["sr_ps", b] = sr_ps
                 for h in range(2):
                     nc.tensor.transpose(
@@ -256,14 +258,6 @@ def tile_rarevariantawarefusion_pa_t_kernel(
                 )
             if part == 2:
                 nc.vector.tensor_tensor(out=m[:, 0, :], in0=m[:, 0, :], in1=m[:, 1, :], op=ALU.max)
-            if part == 4:
-                nc.vector.tensor_scalar(
-                    out=f[:, nsum + w, :, :],
-                    in0=m[:, 0, :].rearrange("p (m t) -> p t m", t=4),
-                    scalar1=24.0 / 7.0,
-                    scalar2=None,
-                    op0=ALU.mult,
-                )
 
         def widen(n, q):
             w = widened(n)
@@ -274,12 +268,23 @@ def tile_rarevariantawarefusion_pa_t_kernel(
                     in_=by_column(tl["r", n][:, 2 * nsum + q : 2 * nsum + q + 2, :]),
                 )
 
+        def widen_max(n):
+            w = widened(n)
+            nc.scalar.mul(
+                out=tl["f", n][:, (NK - w) // 2 + w, :, :],
+                in_=tl["m", n][:, 0, :].rearrange("p (m t) -> p t m", t=4),
+                mul=24.0 / 7.0,
+            )
+
+        def open_sums(n, warm):
+            acc_ps = psum.tile([P, 4, 128], F32, tag="acc", bufs=2, name="acc_ps")
+            tl["acc", n] = acc_ps
+            if warm:
+                keep_warm(acc_ps[:].rearrange("p t i -> p (t i)"))
+
         def add_up(n, ts):
             f = tl["f", n]
             planes = (NK - widened(n)) // 2 + widened(n) + 1
-            if 0 in ts:
-                acc_ps = psum.tile([P, 4, 128], F32, tag="acc", bufs=2, name="acc_ps")
-                tl["acc", n] = acc_ps
             acc_ps = tl["acc", n]
             for t in ts:
                 for q in range(planes):
@@ -292,9 +297,14 @@ def tile_rarevariantawarefusion_pa_t_kernel(
                         stop=(q == planes - 1),
                     )
 
-        def turn_orig(n):
-            o_ps = psum.tile([P, 2, 128], F32, tag="o", bufs=1, name="o_ps")
+        def open_orig(n, warm):
+            o_ps = psum.tile([P, 4, 128], F32, tag="o", bufs=1, name="o_ps")
             tl["o_ps", n] = o_ps
+            if warm:
+                keep_warm(o_ps[:].rearrange("p u i -> p (u i)"))
+
+        def turn_orig(n):
+            o_ps = tl["o_ps", n]
             o_words = tl["o", n][:].bitcast(F32)
             for u in range(2):
                 nc.tensor.transpose(o_ps[:, u, :], o_words[:, u:256:2], ident_f[:])
@@ -308,7 +318,7 @@ def tile_rarevariantawarefusion_pa_t_kernel(
                 in1=s_rows[:, n, :].unsqueeze(2).to_broadcast([P, 128, 4]),
                 op=ALU.mult,
             )
-            nc.scalar.copy(out=g[:, 0, :, :].bitcast(F32), in_=tl["o_ps", n][:].rearrange("p u i -> p i u"))
+            nc.scalar.copy(out=g[:, 0, :, :].bitcast(F32), in_=tl["o_ps", n][:, 0:2, :].rearrange("p u i -> p i u"))
 
         def quantise(n):
             gc = work.tile([P, 256], U32, name="gc", align_bytes=64)
@@ -319,16 +329,22 @@ def tile_rarevariantawarefusion_pa_t_kernel(
                 out=gc[:].bitcast(FP8X4), scales=gs[:], in_=tl["g", n][:].rearrange("p g i t -> p (g i t)")
             )
 
-        def open_product(n):
-            y_ps = psum.tile([P, 2, 256], F32, tag="y", bufs=1, name="y_ps")
-            tl["y", n] = y_ps
-            if n < NPAIR - 1:
-                keep_warm(y_ps[:].rearrange("p h n -> p (h n)"))
+        def keep_warm(bank):
+            nc.tensor.matmul_mx(
+                out=bank,
+                lhsT=wc[:, 0, 0:128].bitcast(FP8X4),
+                lhsT_scale=ws[:, 0, 0:128],
+                rhs=wc[:, 0, :].bitcast(FP8X4),
+                rhs_scale=ws[:, 0, :],
+                start=True,
+                stop=True,
+            )
 
-        def multiply(n):
+        def multiply(n, tag="y", bufs=1):
             gc = tl["gc", n]
             gs = tl["gs", n]
-            y_ps = tl["y", n]
+            y_ps = psum.tile([P, 2, 256], F32, tag=tag, bufs=bufs, name="y_ps")
+            tl["y", n] = y_ps
             for gi in range(2):
                 nc.tensor.matmul_mx(
                     out=y_ps[:].rearrange("p h n -> p (h n)"),
@@ -340,21 +356,9 @@ def tile_rarevariantawarefusion_pa_t_kernel(
                     stop=(gi == 1),
                 )
 
-        def keep_warm(bank):
-            for i in range(2):
-                nc.tensor.matmul_mx(
-                    out=bank,
-                    lhsT=wc[:, i, 0:128].bitcast(FP8X4),
-                    lhsT_scale=ws[:, i, 0:128],
-                    rhs=wc[:, i, :].bitcast(FP8X4),
-                    rhs_scale=ws[:, i, :],
-                    start=True,
-                    stop=True,
-                )
-
         def bias_and_mean(n):
             y_ps = tl["y", n]
-            yb = work.tile([P, 2, 256], F32, name="yb")
+            yb = work.tile([P, 2, 256], F32, name="yb", bufs=4)
             ysum = tiny.tile([P, 2], F32, name="ysum")
             tl["yb", n] = yb
             for hf in range(2):
@@ -385,23 +389,20 @@ def tile_rarevariantawarefusion_pa_t_kernel(
                 )
 
         def inverse_deviation(n):
+            negmu = tiny.tile([P, 2], F32, name="negmu")
+            nc.gpsimd.tensor_scalar(
+                out=negmu[:], in0=tl["ysum", n][:], scalar1=-1.0 / 256.0, scalar2=0.0, op0=ALU.mult, op1=ALU.add
+            )
             ve = tiny.tile([P, 2], F32, name="ve")
-            nc.vector.tensor_scalar(
+            nc.gpsimd.tensor_scalar(
                 out=ve[:], in0=tl["ssq", n][:], scalar1=2.0**-24, scalar2=1e-5, op0=ALU.mult, op1=ALU.add
             )
             rstd = tiny.tile([P, 2], F32, name="rstd")
             nc.gpsimd.tensor_tensor(out=rstd[:], in0=ve[:], in1=half_n[:], op=ALU.pow)
-            tl["rstd", n] = rstd
             nmr = tiny.tile([P, 2], F32, name="nmr")
-            nc.gpsimd.tensor_tensor(out=nmr[:], in0=tl["negmu", n][:], in1=rstd[:], op=ALU.mult)
+            nc.gpsimd.tensor_tensor(out=nmr[:], in0=negmu[:], in1=rstd[:], op=ALU.mult)
+            tl["rstd", n] = rstd
             tl["nmr", n] = nmr
-
-        def negative_mean(n):
-            negmu = tiny.tile([P, 2], F32, name="negmu")
-            nc.vector.tensor_scalar(
-                out=negmu[:], in0=tl["ysum", n][:], scalar1=-1.0 / 256.0, scalar2=None, op0=ALU.mult
-            )
-            tl["negmu", n] = negmu
 
         def normalise(n):
             yb = tl["yb", n]
@@ -425,7 +426,7 @@ def tile_rarevariantawarefusion_pa_t_kernel(
                     nc.tensor.transpose(zt_ps[:, dh, hf, :], z[:, hf, dh * 128 : (dh + 1) * 128], ident_f[:])
 
         def gelu(n):
-            get = work.tile([P, 2, 2, 128], F32, name="get", bufs=4)
+            get = work.tile([P, 2, 2, 128], F32, name="get", bufs=12)
             tl["get", n] = get
             for dh in range(2):
                 nc.scalar.activation(
@@ -462,86 +463,130 @@ def tile_rarevariantawarefusion_pa_t_kernel(
                 cols = slice((n % 2) * 512, (n % 2 + 1) * 512)
                 nc.sync.dma_start(out=outv[n // 2, :, cols], in_=res[:].rearrange("p h d -> p (h d)"))
 
+        def end(p):
+            turn_back(p)
+            residual_and_store(p, 0)
+            residual_and_store(p, 1)
+
         def on(n):
             return 0 <= n < NPAIR
 
-        for n in range(NPAIR + L_RES + 1):
+        for n in range(NPAIR):
             steps = GATE_STEPS.get(n, ())
-            back = [p for p in range(NPAIR) if gelu_slot(p) == n - 1]
             gelus = [p for p in range(NPAIR) if gelu_slot(p) == n]
             turns = [p for p in range(NPAIR) if gelu_slot(p) == n + 1]
+            warm = 2 < n
             if on(n + AHEAD):
                 load(n + AHEAD)
             if n in (0, 1):
                 load_h(4 + 2 * n)
             if n == 0:
                 small_vectors()
+                nc.scalar.copy(out=wg[:], in_=wst[:].rearrange("p g t n -> p g n t"))
+                open_sums(0, False)
+            if on(n - L_Y):
+                multiply(n - L_Y)
+            for j in steps[:1]:
+                gate_tensor(j)
             if on(n):
                 max_and_sums(n, 0)
-            if on(n - L_NORM):
-                inverse_deviation(n - L_NORM)
-            for p in back:
-                turn_back(p)
-            if steps:
-                gate_tensor(steps[0])
-            last = n == NPAIR - 1
             if on(n - L_Q):
                 leave_psum(n - L_Q)
-            if n == 2:
+            if n == 1:
                 spread_weights()
-            if on(n - L_Q - 1):
-                bias_and_mean(n - L_Q - 1)
-            if on(n - L_Q):
-                quantise(n - L_Q)
-            if on(n - L_Q - 1):
-                negative_mean(n - L_Q - 1)
-            if not last:
-                for p in back:
-                    residual_and_store(p, 0)
             if on(n):
                 max_and_sums(n, 1)
-            if not last:
-                for p in back:
-                    residual_and_store(p, 1)
+            if on(n - L_Q):
+                quantise(n - L_Q)
             if n == 0:
                 af_product()
-            if on(n):
-                max_and_sums(n, 3)
-                max_and_sums(n, 2)
-                if last:
-                    for p in back:
-                        residual_and_store(p, 0)
-                max_and_sums(n, 4)
-            if last:
-                for p in back:
-                    residual_and_store(p, 1)
-            if n == 1:
+            max_and_sums(n, 2)
+            max_and_sums(n, 3)
+            if on(n - L_Y):
+                bias_and_mean(n - L_Y)
+            if n == 0:
                 weights()
-            for p in gelus:
-                gelu(p)
-            if steps:
-                gate_scalar(steps[0])
+            if on(n - L_SQ):
+                squares(n - L_SQ)
+                inverse_deviation(n - L_SQ)
+            for j in steps[:1]:
+                gate_scalar(j)
             if n == 0:
                 af_weight()
             for j in steps[1:]:
                 gate_tensor(j)
-            if on(n - 1):
-                add_up(n - 1, (0, 1, 2, 3))
-                turn_orig(n - 1)
-            if on(n - L_Q):
-                open_product(n - L_Q)
-                multiply(n - L_Q)
-            if on(n):
-                widen(n, 0)
-            if on(n - L_Q - 1):
-                squares(n - L_Q - 1)
-            for j in steps[1:]:
                 gate_scalar(j)
-            if on(n):
-                widen(n, 2)
+            if on(n - 1):
+                add_up(n - 1, (0, 1))
+                open_orig(n - 1, warm)
+            if on(n - L_END):
+                end(n - L_END)
+            if on(n - 1):
+                add_up(n - 1, (2, 3))
+                turn_orig(n - 1)
+            if on(n + 1) and n > 0:
+                open_sums(n, warm)
+            widen(n, 0)
+            for p in gelus:
+                gelu(p)
+            widen(n, 2)
+            widen_max(n)
             if on(n - L_NORM):
                 normalise(n - L_NORM)
-            for p, tag in zip(turns, ("zt", "z1")):
-                turn(p, tag)
-            if n == 0:
-                nc.scalar.copy(out=wg[:], in_=wst[:].rearrange("p g t n -> p g n t"))
+            if on(n + 1):
+                for p, tag in zip(turns, ("zt", "z1")):
+                    turn(p, tag)
+
+        last = NPAIR - 1
+        rest = list(range(NPAIR - L_END, NPAIR))
+        leave_psum(last - 1)
+        squares(last - 3)
+        inverse_deviation(last - 3)
+        quantise(last - 1)
+        open_sums(last, True)
+        add_up(last, (0, 1, 2, 3))
+        open_orig(last, False)
+        turn_orig(last)
+        multiply(last - 2)
+        turn(last - 5, "zt")
+        normalise(last - 4)
+        leave_psum(last)
+        bias_and_mean(last - 2)
+        quantise(last)
+        gelu(last - 5)
+        end(rest[0])
+        end(rest[1])
+        squares(last - 2)
+        inverse_deviation(last - 2)
+        multiply(last - 1)
+        multiply(last, "acc", 2)
+        bias_and_mean(last - 1)
+        bias_and_mean(last)
+        turn(last - 4, "z1")
+        squares(last - 1)
+        inverse_deviation(last - 1)
+        normalise(last - 3)
+        squares(last)
+        inverse_deviation(last)
+        end(rest[2])
+        end(rest[3])
+        end(rest[4])
+        end(rest[5])
+        gelu(last - 4)
+        normalise(last - 2)
+        turn(last - 3, "zt")
+        end(last - 5)
+        turn(last - 2, "z1")
+        gelu(last - 3)
+        normalise(last - 1)
+        end(last - 4)
+        gelu(last - 2)
+        turn(last - 1, "zt")
+        normalise(last)
+        end(last - 3)
+        turn(last, "z1")
+        gelu(last - 1)
+        end(last - 2)
+        gelu(last)
+        end(last - 1)
+        end(last)

from contextlib import ExitStack

import concourse.mybir as mybir
from concourse.masks import make_identity

FLOPS = 2 * 4096 * 128 * 256 + 2 * 4096 * 512 * 256

F32 = mybir.dt.float32
BF16 = mybir.dt.bfloat16
U32 = mybir.dt.uint32
I32 = mybir.dt.int32
U8 = mybir.dt.uint8
FP8X4 = mybir.dt.float8_e4m3fn_x4
ALU = mybir.AluOpType
ACT = mybir.ActivationFunctionType

P = 128
NB = 8
NK = 8
D = 256
NPAIR = 16
AHEAD = 2
GATE_STEPS = {0: (0, 1), **{n: (n + 1,) for n in range(1, NB + 1)}}
L_Q = 2
L_Y = 3
L_SQ = 4
L_NORM = 5
L_GELU = 6
L_END = 12
GELU_FROM = NB


def widened(n):
    return 0 if n == 0 else 2 if n < GELU_FROM + 2 else 4


def gelu_slot(n):
    return max(n + L_GELU, GELU_FROM + n // 2)


def tile_rarevariantawarefusion_pa_t_kernel(
    tc, orig_feat, rag_feat, af, h_af, w2, b2, wf, bias_f, ln_g, ln_b, out
):
    nc = tc.nc
    with ExitStack() as ctx:
        const = ctx.enter_context(tc.tile_pool(name="const", bufs=1))
        s1 = ctx.enter_context(tc.tile_pool(name="s1", bufs=2))
        rpool = ctx.enter_context(tc.tile_pool(name="rpool", bufs=4))
        opool = ctx.enter_context(tc.tile_pool(name="opool", bufs=16))
        fpool = ctx.enter_context(tc.tile_pool(name="fpool", bufs=3))
        work = ctx.enter_context(tc.tile_pool(name="work", bufs=3))
        tiny = ctx.enter_context(tc.tile_pool(name="tiny", bufs=6))
        psum = ctx.enter_context(tc.psum_pool(name="psum", bufs=1))
        ctx.enter_context(tc.manual_schedule())

        rv = rag_feat.rearrange("b k (i c) d -> b i k (c d)", c=4)
        ov = orig_feat.rearrange("b (i c) d -> b i (c d)", c=4)
        outv = out.rearrange("b (i c) d -> b i (c d)", c=4)
        tl = {}

        def load(n):
            cols = slice((n % 2) * 512, (n % 2 + 1) * 512)
            r = rpool.tile([P, NK, 512], BF16, name="r")
            for ks in ((0, 4, 2, 6) if n == 0 else (0,)):
                k1 = ks + (2 if n == 0 else NK)
                nc.sync.dma_start(out=r[:, ks:k1, :], in_=rv[n // 2, :, ks:k1, cols])
            o = opool.tile([P, 512], BF16, name="o")
            nc.sync.dma_start(out=o[:], in_=ov[n // 2, :, cols])
            tl["r", n] = r
            tl["o", n] = o

        def load_h(b):
            h = const.tile([P, 2, 4, 128], BF16, name="h%d" % b)
            nc.sync.dma_start(
                out=h[:].rearrange("p b c h -> p b (c h)"),
                in_=h_af[b : b + 2].rearrange("b (i c) h -> i b (c h)", c=4),
            )
            for i in range(2):
                tl["h", b + i] = h[:, i, :, :]

        a_bf = const.tile([P, NB, 4], BF16, name="a_bf")
        nc.scalar.dma_start(out=a_bf[:], in_=af.rearrange("b (i c) -> i b c", c=4))
        load(0)
        load_h(0)
        load_h(2)
        for n in range(1, AHEAD):
            load(n)
        w2_sb = const.tile([P, D], BF16, name="w2_sb")
        nc.scalar.dma_start(out=w2_sb[:], in_=w2)
        vrow = const.tile([P, P], BF16, name="vrow")
        nc.vector.memset(vrow[:], 0.0)
        nc.scalar.dma_start(out=vrow[0:2, :], in_=b2.rearrange("(r c) -> r c", r=2))
        nc.scalar.dma_start(out=vrow[2:4, :], in_=ln_g.rearrange("(r c) -> r c", r=2))
        nc.scalar.dma_start(out=vrow[4:6, :], in_=ln_b.rearrange("(r c) -> r c", r=2))
        wst = const.tile([P, 2, 4, 256], BF16, name="wst")
        for half in range(2):
            nc.gpsimd.dma_start(
                out=wst[64 * half : 64 * half + 64, :, :, :].rearrange("p g t n -> p g (t n)"),
                in_=wf.rearrange("(g j t) n -> j g (t n)", g=2, t=4),
            )
        bias_bc = const.tile([P, D], BF16, name="bias_bc")
        nc.gpsimd.dma_start(out=bias_bc[:], in_=bias_f.partition_broadcast(P))

        ident_b = const.tile([P, P], BF16, name="ident_b")
        make_identity(nc, ident_b[:])
        ident_f = const.tile([P, P], F32, name="ident_f")
        make_identity(nc, ident_f[:])
        ones_f = const.tile([P, P], F32, name="ones_f")
        nc.vector.memset(ones_f[:], 1.0)
        half_n = const.tile([P, 2], F32, name="half_n")
        nc.vector.memset(half_n[:], -0.5)
        wcc = const.tile([P, 2, 256], U32, name="wcc", align_bytes=64)
        wsc = const.tile([P, 2, 256], U8, name="wsc", align_bytes=64)
        wc = const.tile([P, 2, 512], U32, name="wc", align_bytes=64)
        ws = const.tile([P, 2, 512], U8, name="ws", align_bytes=64)
        nc.gpsimd.memset(wsc[:].bitcast(U32), 0)
        nc.gpsimd.memset(ws[:].bitcast(U32), 0)
        nc.gpsimd.memset(wc[:], 0)

        a_flat = a_bf[:].rearrange("p b c -> p (b c)")
        a1 = const.tile([P, 32], F32, name="a1")
        wgt = const.tile([P, 32], F32, name="wgt")

        def af_product():
            nc.vector.tensor_scalar(out=a1[:], in0=a_flat, scalar1=-1.0, scalar2=1.0, op0=ALU.mult, op1=ALU.add)
            nc.vector.tensor_tensor(out=a1[:], in0=a1[:], in1=a_flat, op=ALU.mult)

        def af_weight():
            nc.scalar.activation(out=wgt[:], in_=a1[:], func=ACT.Sqrt)

        nc.scalar.activation(out=wgt[:, 0:1], in_=ones_f[:, 0:1], func=ACT.Sqrt)

        vcol = const.tile([P, 8], F32, name="vcol")
        b2rep = const.tile([P, 2, P], F32, name="b2rep")

        def small_vectors():
            vt_ps = psum.tile([P, P], BF16, tag="f", bufs=2, name="vt_ps")
            nc.tensor.transpose(vt_ps[:], vrow[:], ident_b[:])
            nc.scalar.copy(out=vcol[:, 0:6], in_=vt_ps[:, 0:6])
            for dh in range(2):
                nc.scalar.activation(out=b2rep[:, dh, :], in_=ones_f[:], func=ACT.Copy, scale=vcol[:, dh : dh + 1])

        wg = const.tile([P, 2, 256, 4], BF16, name="wg", align_bytes=64)

        def weights():
            nc.vector.quantize_mx(
                out=wcc[:].rearrange("p g n -> p (g n)").bitcast(FP8X4),
                scales=wsc[:].rearrange("p g n -> p (g n)"),
                in_=wg[:].rearrange("p g n t -> p (g n t)"),
            )

        def spread_weights():
            for half in range(2):
                rows = slice(64 * half, 64 * half + 64)
                cols = slice(256 * half, 256 * half + 256)
                nc.vector.tensor_copy(out=wc[rows, :, cols].bitcast(I32), in_=wcc[rows, :, :].bitcast(I32))
                nc.vector.tensor_copy(out=ws[rows, :, cols].bitcast(I32), in_=wsc[rows, :, :].bitcast(I32))

        s_sb = const.tile([P, 32], F32, name="s_sb")
        s_rows = const.tile([P, NPAIR, 128], F32, name="s_rows")

        def gate_tensor(j):
            if j < NB:
                ht_ps = psum.tile([P, 4, 128], BF16, tag="f", bufs=2, name="ht_ps")
                for c in range(4):
                    nc.tensor.transpose(ht_ps[:, c, :], tl["h", j][:, c, :], ident_b[:])
                tl["ht_ps", j] = ht_ps
            if 0 <= j - 1 < NB:
                b = j - 1
                for cp in range(2):
                    z_ps = psum.tile([P, 2, D], F32, tag=("z1", "f")[cp], bufs=(1, 2)[cp], name="z_ps")
                    tl["z_ps", b, cp] = z_ps
                    for ci in range(2):
                        c = 2 * cp + ci
                        nc.tensor.matmul(
                            z_ps[:, ci, :],
                            lhsT=tl["ht", b][:, c * 128 : (c + 1) * 128],
                            rhs=w2_sb[:],
                            start=True,
                            stop=False,
                        )
                        for dh in range(2):
                            nc.tensor.matmul(
                                z_ps[:, ci, dh * 128 : (dh + 1) * 128],
                                lhsT=b2rep[:, dh, :],
                                rhs=ident_f[:],
                                is_transpose=True,
                                start=False,
                                stop=(dh == 1),
                            )
            if 0 <= j - 2 < NB:
                b = j - 2
                sr_ps = psum.tile([P, 2, 128], F32, tag="zt" if j <= NB else "f", bufs=1 if j <= NB else 2, name="sr_ps")
                tl["sr_ps", b] = sr_ps
                for h in range(2):
                    nc.tensor.transpose(
                        sr_ps[:, h, :],
                        tl["srep", b][:, 2 * h : 2 * h + 2, :].rearrange("p c j -> p (c j)"),
                        ident_f[:],
                    )

        def gate_scalar(j):
            if j < NB:
                ht = s1.tile([P, 512], BF16, name="ht")
                nc.scalar.copy(out=ht[:], in_=tl["ht_ps", j][:].rearrange("p c i -> p (c i)"))
                tl["ht", j] = ht
            if 0 <= j - 1 < NB:
                b = j - 1
                for c in range(4):
                    sjunk = s1.tile([P, D], BF16, name="sjunk")
                    nc.scalar.activation(
                        out=sjunk[:],
                        in_=tl["z_ps", b, c // 2][:, c % 2, :],
                        func=ACT.Sigmoid,
                        accum_out=s_sb[:, b * 4 + c : b * 4 + c + 1],
                    )
            if 0 <= j - 2 < NB:
                b = j - 2
                nc.scalar.copy(out=s_rows[:, 2 * b : 2 * b + 2, :], in_=tl["sr_ps", b][:])
            if 0 <= j - 1 < NB:
                b = j - 1
                srep = s1.tile([P, 4, 64], F32, name="srep")
                tl["srep", b] = srep
                nc.scalar.mul(
                    out=srep[:],
                    in_=s_sb[:, b * 4 : (b + 1) * 4].unsqueeze(2).to_broadcast([P, 4, 64]),
                    mul=0.7 / 8.0,
                )

        def by_column(ap):
            return ap.rearrange("p k (m t) -> p k t m", t=4)

        def max_and_sums(n, part):
            r = tl["r", n]
            w = widened(n)
            nsum = (NK - w) // 2
            if part == 0:
                m = work.tile([P, 4, 512], BF16, name="m", bufs=2)
                f = fpool.tile([P, 7, 4, 128], F32, name="f")
                tl["m", n] = m
                tl["f", n] = f
            m = tl["m", n]
            f = tl["f", n]
            if part == 0:
                step = 2 if n == 0 else 4
                for k in range(0, 4, step):
                    nc.vector.tensor_tensor(
                        out=m[:, k : k + step, :], in0=r[:, k : k + step, :], in1=r[:, k + 4 : k + 4 + step, :], op=ALU.max
                    )
            if part == 1:
                nc.vector.tensor_tensor(out=m[:, 0:2, :], in0=m[:, 0:2, :], in1=m[:, 2:4, :], op=ALU.max)
            if part == 3:
                nc.vector.tensor_tensor(
                    out=f[:, 0:nsum, :, :],
                    in0=by_column(r[:, 0:nsum, :]),
                    in1=by_column(r[:, nsum : 2 * nsum, :]),
                    op=ALU.add,
                )
            if part == 2:
                nc.vector.tensor_tensor(out=m[:, 0, :], in0=m[:, 0, :], in1=m[:, 1, :], op=ALU.max)

        def widen(n, q):
            w = widened(n)
            nsum = (NK - w) // 2
            if q < w:
                nc.scalar.copy(
                    out=tl["f", n][:, nsum + q : nsum + q + 2, :, :],
                    in_=by_column(tl["r", n][:, 2 * nsum + q : 2 * nsum + q + 2, :]),
                )

        def widen_max(n):
            w = widened(n)
            nc.scalar.mul(
                out=tl["f", n][:, (NK - w) // 2 + w, :, :],
                in_=tl["m", n][:, 0, :].rearrange("p (m t) -> p t m", t=4),
                mul=24.0 / 7.0,
            )

        def open_sums(n, warm):
            acc_ps = psum.tile([P, 4, 128], F32, tag="acc", bufs=2, name="acc_ps")
            tl["acc", n] = acc_ps
            if warm:
                keep_warm(acc_ps[:].rearrange("p t i -> p (t i)"))

        def add_up(n, ts):
            f = tl["f", n]
            planes = (NK - widened(n)) // 2 + widened(n) + 1
            acc_ps = tl["acc", n]
            for t in ts:
                for q in range(planes):
                    nc.tensor.matmul(
                        acc_ps[:, t, :],
                        lhsT=f[:, q, t, :],
                        rhs=ident_f[:],
                        is_transpose=True,
                        start=(q == 0),
                        stop=(q == planes - 1),
                    )

        def open_orig(n, warm):
            o_ps = psum.tile([P, 4, 128], F32, tag="o", bufs=1, name="o_ps")
            tl["o_ps", n] = o_ps
            if warm:
                keep_warm(o_ps[:].rearrange("p u i -> p (u i)"))

        def turn_orig(n):
            o_ps = tl["o_ps", n]
            o_words = tl["o", n][:].bitcast(F32)
            for u in range(2):
                nc.tensor.transpose(o_ps[:, u, :], o_words[:, u:256:2], ident_f[:])

        def leave_psum(n):
            g = work.tile([P, 2, 128, 4], BF16, name="g", align_bytes=64)
            tl["g", n] = g
            nc.vector.tensor_tensor(
                out=g[:, 1, :, :],
                in0=tl["acc", n][:].rearrange("p t i -> p i t"),
                in1=s_rows[:, n, :].unsqueeze(2).to_broadcast([P, 128, 4]),
                op=ALU.mult,
            )
            nc.scalar.copy(out=g[:, 0, :, :].bitcast(F32), in_=tl["o_ps", n][:, 0:2, :].rearrange("p u i -> p i u"))

        def quantise(n):
            gc = work.tile([P, 256], U32, name="gc", align_bytes=64)
            gs = work.tile([P, 256], U8, name="gs", align_bytes=64)
            tl["gc", n] = gc
            tl["gs", n] = gs
            nc.vector.quantize_mx(
                out=gc[:].bitcast(FP8X4), scales=gs[:], in_=tl["g", n][:].rearrange("p g i t -> p (g i t)")
            )

        def keep_warm(bank):
            nc.tensor.matmul_mx(
                out=bank,
                lhsT=wc[:, 0, 0:128].bitcast(FP8X4),
                lhsT_scale=ws[:, 0, 0:128],
                rhs=wc[:, 0, :].bitcast(FP8X4),
                rhs_scale=ws[:, 0, :],
                start=True,
                stop=True,
            )

        def multiply(n, tag="y", bufs=1):
            gc = tl["gc", n]
            gs = tl["gs", n]
            y_ps = psum.tile([P, 2, 256], F32, tag=tag, bufs=bufs, name="y_ps")
            tl["y", n] = y_ps
            for gi in range(2):
                nc.tensor.matmul_mx(
                    out=y_ps[:].rearrange("p h n -> p (h n)"),
                    lhsT=gc[:, gi * 128 : (gi + 1) * 128].bitcast(FP8X4),
                    lhsT_scale=gs[:, gi * 128 : (gi + 1) * 128],
                    rhs=wc[:, gi, :].bitcast(FP8X4),
                    rhs_scale=ws[:, gi, :],
                    start=(gi == 0),
                    stop=(gi == 1),
                )

        def bias_and_mean(n):
            y_ps = tl["y", n]
            yb = work.tile([P, 2, 256], F32, name="yb", bufs=4)
            ysum = tiny.tile([P, 2], F32, name="ysum")
            tl["yb", n] = yb
            for hf in range(2):
                nc.vector.scalar_tensor_tensor(
                    out=yb[:, hf, :],
                    in0=y_ps[:, hf, :],
                    scalar=1.0,
                    in1=bias_bc[:],
                    op0=ALU.mult,
                    op1=ALU.add,
                    accum_out=ysum[:, hf : hf + 1],
                )
            tl["ysum", n] = ysum

        def squares(n):
            yb = tl["yb", n]
            junk = work.tile([P, 256], BF16, name="junk", bufs=2)
            ssq = tiny.tile([P, 2], F32, name="ssq")
            tl["ssq", n] = ssq
            for hf in range(2):
                nc.scalar.activation(
                    out=junk[:],
                    in_=yb[:, hf, :],
                    func=ACT.Square,
                    scale=-256.0,
                    bias=tl["ysum", n][:, hf : hf + 1],
                    accum_out=ssq[:, hf : hf + 1],
                )

        def inverse_deviation(n):
            negmu = tiny.tile([P, 2], F32, name="negmu")
            nc.gpsimd.tensor_scalar(
                out=negmu[:], in0=tl["ysum", n][:], scalar1=-1.0 / 256.0, scalar2=0.0, op0=ALU.mult, op1=ALU.add
            )
            ve = tiny.tile([P, 2], F32, name="ve")
            nc.gpsimd.tensor_scalar(
                out=ve[:], in0=tl["ssq", n][:], scalar1=2.0**-24, scalar2=1e-5, op0=ALU.mult, op1=ALU.add
            )
            rstd = tiny.tile([P, 2], F32, name="rstd")
            nc.gpsimd.tensor_tensor(out=rstd[:], in0=ve[:], in1=half_n[:], op=ALU.pow)
            nmr = tiny.tile([P, 2], F32, name="nmr")
            nc.gpsimd.tensor_tensor(out=nmr[:], in0=negmu[:], in1=rstd[:], op=ALU.mult)
            tl["rstd", n] = rstd
            tl["nmr", n] = nmr

        def normalise(n):
            yb = tl["yb", n]
            z = work.tile([P, 2, 256], F32, name="z", bufs=5)
            tl["z", n] = z
            for hf in range(2):
                nc.scalar.activation(
                    out=z[:, hf, :],
                    in_=yb[:, hf, :],
                    func=ACT.Identity,
                    scale=tl["rstd", n][:, hf : hf + 1],
                    bias=tl["nmr", n][:, hf : hf + 1],
                )

        def turn(n, tag):
            z = tl["z", n]
            zt_ps = psum.tile([P, 2, 2, 128], F32, tag=tag, bufs=1, name="zt_ps")
            tl["zt", n] = zt_ps
            for dh in range(2):
                for hf in range(2):
                    nc.tensor.transpose(zt_ps[:, dh, hf, :], z[:, hf, dh * 128 : (dh + 1) * 128], ident_f[:])

        def gelu(n):
            get = work.tile([P, 2, 2, 128], F32, name="get", bufs=12)
            tl["get", n] = get
            for dh in range(2):
                nc.scalar.activation(
                    out=get[:, dh, :, :],
                    in_=tl["zt", n][:, dh, :, :],
                    func=ACT.Gelu,
                    scale=vcol[:, 2 + dh : 3 + dh],
                    bias=vcol[:, 4 + dh : 5 + dh],
                )

        def turn_back(n):
            get = tl["get", n]
            f_ps = psum.tile([P, 2, 2, 128], F32, tag="f", bufs=2, name="f_ps")
            tl["f_ps", n] = f_ps
            for hf in range(2):
                for dh in range(2):
                    nc.tensor.transpose(f_ps[:, hf, dh, :], get[:, dh, hf, :], ident_f[:])

        def residual_and_store(n, hf):
            if hf == 0:
                res = work.tile([P, 2, 256], F32, name="res")
                tl["res", n] = res
            res = tl["res", n]
            tau = n * 2 + hf
            nc.vector.scalar_tensor_tensor(
                out=res[:, hf, :],
                in0=tl["f_ps", n][:, hf, :, :].rearrange("p a d -> p (a d)"),
                scalar=wgt[:, tau : tau + 1],
                in1=tl["o", n][:, hf * 256 : (hf + 1) * 256],
                op0=ALU.mult,
                op1=ALU.add,
            )
            if hf == 1:
                cols = slice((n % 2) * 512, (n % 2 + 1) * 512)
                nc.sync.dma_start(out=outv[n // 2, :, cols], in_=res[:].rearrange("p h d -> p (h d)"))

        def end(p):
            turn_back(p)
            residual_and_store(p, 0)
            residual_and_store(p, 1)

        def on(n):
            return 0 <= n < NPAIR

        for n in range(NPAIR):
            steps = GATE_STEPS.get(n, ())
            gelus = [p for p in range(NPAIR) if gelu_slot(p) == n]
            turns = [p for p in range(NPAIR) if gelu_slot(p) == n + 1]
            warm = 2 < n
            if on(n + AHEAD):
                load(n + AHEAD)
            if n in (0, 1):
                load_h(4 + 2 * n)
            if n == 0:
                small_vectors()
                nc.scalar.copy(out=wg[:], in_=wst[:].rearrange("p g t n -> p g n t"))
                open_sums(0, False)
            if on(n - L_Y):
                multiply(n - L_Y)
            for j in steps[:1]:
                gate_tensor(j)
            if on(n):
                max_and_sums(n, 0)
            if on(n - L_Q):
                leave_psum(n - L_Q)
            if n == 1:
                spread_weights()
            if on(n):
                max_and_sums(n, 1)
            if on(n - L_Q):
                quantise(n - L_Q)
            if n == 0:
                af_product()
            max_and_sums(n, 2)
            max_and_sums(n, 3)
            if on(n - L_Y):
                bias_and_mean(n - L_Y)
            if n == 0:
                weights()
            if on(n - L_SQ):
                squares(n - L_SQ)
                inverse_deviation(n - L_SQ)
            for j in steps[:1]:
                gate_scalar(j)
            if n == 0:
                af_weight()
            for j in steps[1:]:
                gate_tensor(j)
                gate_scalar(j)
            if on(n - 1):
                add_up(n - 1, (0, 1))
                open_orig(n - 1, warm)
            if on(n - L_END):
                end(n - L_END)
            if on(n - 1):
                add_up(n - 1, (2, 3))
                turn_orig(n - 1)
            if on(n + 1) and n > 0:
                open_sums(n, warm)
            widen(n, 0)
            for p in gelus:
                gelu(p)
            widen(n, 2)
            widen_max(n)
            if on(n - L_NORM):
                normalise(n - L_NORM)
            if on(n + 1):
                for p, tag in zip(turns, ("zt", "z1")):
                    turn(p, tag)

        last = NPAIR - 1
        rest = list(range(NPAIR - L_END, NPAIR))
        leave_psum(last - 1)
        squares(last - 3)
        inverse_deviation(last - 3)
        quantise(last - 1)
        open_sums(last, True)
        add_up(last, (0, 1, 2, 3))
        open_orig(last, False)
        turn_orig(last)
        multiply(last - 2)
        turn(last - 5, "zt")
        normalise(last - 4)
        leave_psum(last)
        bias_and_mean(last - 2)
        quantise(last)
        gelu(last - 5)
        end(rest[0])
        end(rest[1])
        squares(last - 2)
        inverse_deviation(last - 2)
        multiply(last - 1)
        multiply(last, "acc", 2)
        bias_and_mean(last - 1)
        bias_and_mean(last)
        turn(last - 4, "z1")
        squares(last - 1)
        inverse_deviation(last - 1)
        normalise(last - 3)
        squares(last)
        inverse_deviation(last)
        end(rest[2])
        end(rest[3])
        end(rest[4])
        end(rest[5])
        gelu(last - 4)
        normalise(last - 2)
        turn(last - 3, "zt")
        end(last - 5)
        turn(last - 2, "z1")
        gelu(last - 3)
        normalise(last - 1)
        end(last - 4)
        gelu(last - 2)
        turn(last - 1, "zt")
        normalise(last)
        end(last - 3)
        turn(last, "z1")
        gelu(last - 1)
        end(last - 2)
        gelu(last)
        end(last - 1)
        end(last)
